import numpy as np
import ml_dtypes


def mxq(x, axis, fmt="e4m3"):
    dtype, down = {"e4m3": (ml_dtypes.float8_e4m3fn, 7), "e5m2": (ml_dtypes.float8_e5m2, 14)}[fmt]
    v = np.moveaxis(np.asarray(x, np.float32).astype(ml_dtypes.bfloat16).astype(np.float64), axis, -1)
    blocks = v.reshape(v.shape[:-1] + (-1, 32))
    amax = np.abs(blocks).max(-1, keepdims=True)
    byte = np.maximum(np.where(amax > 0, np.frexp(amax)[1] - 1 + 127, 0) - down, 1)
    scale = np.exp2(byte - 127.0)
    codes = (blocks / scale).astype(np.float32).astype(dtype).astype(np.float64)
    return np.moveaxis((codes * scale).reshape(v.shape), -1, axis)


WIDE = False


def mx_kscale(k):
    if not WIDE:
        return np.ones(k)
    levels = np.array([10, -10, 5, -5, 0])
    a = np.random.permutation(np.resize(levels, k // 512 * 4)).reshape(k // 512, 4)
    idx = np.arange(k)
    return np.exp2(a[idx // 512, idx % 128 // 32])


BF16 = ml_dtypes.bfloat16


def bf(x):
    return np.asarray(x, np.float32).astype(BF16)


def f64(x):
    return np.asarray(x).astype(np.float64)


E2M1 = np.array([0.0, 0.5, 1.0, 1.5, 2.0, 3.0, 4.0, 6.0, -0.0, -0.5, -1.0, -1.5, -2.0, -3.0, -4.0, -6.0])


def pack_weight(w, fmt):
    k, n = w.shape
    w = f64(bf(w)).reshape(k // 32, 32, n)
    amax = np.abs(w).max(1)
    if fmt == "e4m3":
        byte = np.frexp(amax)[1] - 1 + 127 - 7
    else:
        mant, ex = np.frexp(amax / 6.0)
        byte = np.where(mant > 0.5, ex, ex - 1) + 127
    byte = np.clip(np.where(amax > 0, byte, 1), 1, 254)
    scaled = (w * np.exp2(127.0 - byte)[:, None, :]).reshape(k, n).astype(np.float32)
    by_word = np.ascontiguousarray(scaled.reshape(k // 512, 128, 4, n).transpose(0, 1, 3, 2))
    if fmt == "e4m3":
        words = by_word.astype(ml_dtypes.float8_e4m3fn).view(np.uint8)
    else:
        c = by_word.astype(ml_dtypes.float4_e2m1fn).view(np.uint8) & 0xF
        words = c[..., 0::2] | (c[..., 1::2] << 4)
    return np.ascontiguousarray(words), np.ascontiguousarray(byte.astype(np.uint8).reshape(k // 512, 16, n))


def unpack_weight(words, scales, fmt):
    g, p, n, _ = words.shape
    if fmt == "e4m3":
        vals = np.ascontiguousarray(words).view(ml_dtypes.float8_e4m3fn).astype(np.float64)
    else:
        nib = np.empty((g, p, n, 4), np.uint8)
        nib[..., 0::2] = words & 0xF
        nib[..., 1::2] = words >> 4
        vals = E2M1[nib]
    vals = vals * np.repeat(np.exp2(scales.astype(np.float64) - 127.0), 8, axis=1)[..., None]
    return vals.transpose(0, 1, 3, 2).reshape(g * 512, n)


B, S, C, H, D = 4, 512, 1024, 8, 128
E = H * D
EPS = 1e-15
FMT = "e4m3"


def setup_inputs():
    t = mx_kscale(E)
    q_feat = bf(np.maximum(np.random.standard_normal((B, H, S, D)), 0.0))
    vk = bf(np.random.standard_normal((B, H, D, D)) * np.sqrt(S) * t.reshape(H, D)[None, :, :, None])
    k_sum = bf(S * (0.11 + 0.02 * np.random.standard_normal((B, H, D))))
    wo = np.random.standard_normal((C, E)) * 6.0 / np.sqrt(E) / t[None, :]
    words, scales = pack_weight(np.ascontiguousarray(wo.T), FMT)
    bo = bf(np.random.standard_normal(C) * 0.1)
    return {"q_feat": q_feat,
            "vk": vk,
            "k_sum": k_sum,
            "Wo_words": words,
            "Wo_scales": scales,
            "bo": bo}


def reference(q_feat, vk, k_sum, Wo_words, Wo_scales, bo):
    hs = f64(vk) @ f64(q_feat).transpose(0, 1, 3, 2)
    den = (f64(q_feat) * f64(k_sum)[:, :, None, :]).sum(-1)
    hs = hs / (den[:, :, None, :] + EPS)
    a = hs.transpose(0, 3, 1, 2).reshape(B, S, E)
    return (mxq(a, 2, "e4m3") @ unpack_weight(Wo_words, Wo_scales, FMT)) + f64(bo)

@@ -1,0 +1,242 @@
+from contextlib import ExitStack
+
+import concourse.mybir as mybir
+from concourse.masks import make_identity
+
+F32 = mybir.dt.float32
+BF16 = mybir.dt.bfloat16
+I32 = mybir.dt.int32
+U32 = mybir.dt.uint32
+U8 = mybir.dt.uint8
+FP8X4 = mybir.dt.float8_e4m3fn_x4
+ALU = mybir.AluOpType
+ACT = mybir.ActivationFunctionType
+
+B, H, S, D = 4, 8, 512, 128
+C = 1024
+P = 128
+EPS = 1e-15
+PACK = 4
+K_PASS = P * PACK
+PASSES = H * D // K_PASS
+HEADS_PER_PASS = K_PASS // D
+N_MX = 512
+N_HALVES = C // N_MX
+ROWS = S // P
+TILES = B * ROWS
+VK_PITCH = 136
+
+BANK_HEADS = ((0, 1, 2), (4, 5, 6), (3, 7))
+
+FLOPS = 2 * B * S * (H * D) * C + 2 * B * H * S * D * D + 2 * B * H * S * D
+
+
+def tile_lineartransformerblock_pc_kernel(tc, q_feat, vk, k_sum, Wo_words, Wo_scales, bo, out):
+    nc = tc.nc
+    with ExitStack() as ctx:
+        keep = ctx.enter_context(tc.tile_pool(name="keep", bufs=1))
+        work = ctx.enter_context(tc.tile_pool(name="work", bufs=3))
+        ps_t = ctx.enter_context(tc.psum_pool(name="ps_t", bufs=2))
+        ps_one = ctx.enter_context(tc.psum_pool(name="ps_one", bufs=1))
+        ctx.enter_context(tc.manual_schedule())
+
+        q_sb = [keep.tile([P, H, ROWS, D], BF16, name="q_sb%d" % b) for b in range(B)]
+        vk_sb = [keep.tile([P, H, D], BF16, name="vk_sb%d" % b) for b in range(B)]
+        ks_sb = keep.tile([P, P], BF16, name="ks_sb")
+        bias_row = keep.tile([P, C], BF16, name="bias_row")
+        w_words = keep.tile([P, PASSES, C * PACK], U8, name="w_words", align_bytes=64)
+        w_scales = keep.tile([P, PASSES, C], U8, name="w_scales", align_bytes=64)
+
+        nc.vector.memset(ks_sb[:], 0.0)
+        nc.vector.memset(bias_row[:], 0.0)
+        nc.vector.memset(w_scales[:].rearrange("p g n -> p (g n)").bitcast(I32), 0)
+
+        def load_q(b, half):
+            heads = slice(half * HEADS_PER_PASS, (half + 1) * HEADS_PER_PASS)
+            nc.sync.dma_start(
+                out=q_sb[b][:, heads, :, :].rearrange("p h r d -> p h (r d)"),
+                in_=q_feat[b, heads].rearrange("h (p r) d -> p h (r d)", r=ROWS),
+            )
+
+        def load_vk(b):
+            nc.sync.dma_start(out=vk_sb[b][:], in_=vk[b].rearrange("h n d -> n h d"))
+
+        load_q(0, 0)
+        load_vk(0)
+        load_q(0, 1)
+        nc.sync.dma_start(out=ks_sb[0 : B * H, :], in_=k_sum.rearrange("b h d -> (b h) d"))
+        nc.sync.dma_start(out=bias_row[0:1, :], in_=bo.rearrange("(o c) -> o c", o=1))
+        for quad in range(4):
+            nc.sync.dma_start(
+                out=w_scales[32 * quad : 32 * quad + 4, :, :].bitcast(I32),
+                in_=Wo_scales[:, 4 * quad : 4 * quad + 4, :].rearrange("g r n -> r g n").bitcast(I32),
+            )
+        for g in range(PASSES):
+            nc.sync.dma_start(
+                out=w_words[:, g, :].bitcast(I32),
+                in_=Wo_words[g].rearrange("p n t -> p (n t)").bitcast(I32),
+            )
+        for b in range(1, B):
+            load_vk(b)
+            load_q(b, 0)
+            load_q(b, 1)
+
+        ident_bf = keep.tile([P, P], BF16, name="ident_bf")
+        make_identity(nc, ident_bf[:])
+        ident_f32 = keep.tile([P, P], F32, name="ident_f32")
+        make_identity(nc, ident_f32[:])
+        ones_bf = keep.tile([P, P], BF16, name="ones_bf")
+        nc.vector.memset(ones_bf[:], 1.0)
+        order_n = keep.tile([P, P], BF16, name="order_n")
+        nc.vector.tensor_copy(
+            out=order_n[:].rearrange("p (u j e) -> p u j e", u=2, j=32, e=2),
+            in_=ident_bf[:].rearrange("p (j u e) -> p u j e", j=32, u=2, e=2),
+        )
+
+        bias_sb = keep.tile([P, C], F32, name="bias_sb")
+        for nh in range(N_HALVES):
+            cols = slice(nh * N_MX, (nh + 1) * N_MX)
+            bias_ps = ps_one.tile([P, N_MX], F32, name="bias_ps", tag="o%d" % nh)
+            nc.tensor.matmul(out=bias_ps[:], lhsT=ones_bf[:], rhs=bias_row[:, cols], start=True, stop=True)
+            nc.vector.tensor_copy(out=bias_sb[:, cols], in_=bias_ps[:])
+
+        vk_t = keep.tile([P, B * H, VK_PITCH], BF16, name="vk_t")
+        ks_ps = ps_t.tile([P, H, P], BF16, name="ks_ps", tag="t")
+        nc.tensor.transpose(out=ks_ps[:, 0, :], in_=ks_sb[:], identity=ident_bf[:])
+        nc.scalar.copy(out=vk_t[:, :, D], in_=ks_ps[:, 0, 0 : B * H])
+
+        def transpose_vk(b):
+            vk_ps = ps_t.tile([P, H, P], BF16, name="vk_ps", tag="t")
+            for h in range(H):
+                nc.tensor.transpose(out=vk_ps[:, h, :], in_=vk_sb[b][:, h, :], identity=order_n[:])
+            nc.scalar.copy(out=vk_t[:, b * H : (b + 1) * H, 0:D], in_=vk_ps[:])
+
+        q_t = {}
+        hs_ps = {}
+        r_den = {}
+        a_sb = {}
+        grouped = {}
+        codes = {}
+        a_scales = {}
+        out_ps = {}
+
+        def transpose_q(i):
+            b, r = divmod(i, ROWS)
+            q_ps = ps_t.tile([P, H, P], BF16, name="q_ps", tag="t")
+            for h in range(H):
+                nc.tensor.transpose(out=q_ps[:, h, :], in_=q_sb[b][:, h, r, :], identity=ident_bf[:])
+            q_t[i] = work.tile([P, H, P], BF16, name="q_t")
+            nc.scalar.copy(out=q_t[i][:], in_=q_ps[:])
+
+        def read_out(i):
+            b = i // ROWS
+            hs_ps[i] = []
+            den = work.tile([P, H], F32, name="den")
+            for k, heads in enumerate(BANK_HEADS):
+                bank = ps_one.tile([P, 3, D + 1], F32, name="hs_ps", tag="hs%d" % k)
+                for slot, h in enumerate(heads):
+                    nc.tensor.matmul(
+                        out=bank[:, slot, :],
+                        lhsT=q_t[i][:, h, :],
+                        rhs=vk_t[:, b * H + h, 0 : D + 1],
+                        start=True,
+                        stop=True,
+                    )
+                hs_ps[i].append(bank)
+            for k, heads in enumerate(BANK_HEADS):
+                nc.vector.tensor_scalar_add(
+                    out=den[:, 3 * k : 3 * k + len(heads)], in0=hs_ps[i][k][:, 0 : len(heads), D], scalar1=EPS
+                )
+            r_den[i] = work.tile([P, H], F32, name="r_den")
+            nc.vector.reciprocal(out=r_den[i][:], in_=den[:])
+
+        def normalise(i):
+            a_sb[i] = work.tile([P, PASSES, 2, HEADS_PER_PASS, D // 2], BF16, name="a_sb")
+            for k in range(2):
+                for slot, h in enumerate(BANK_HEADS[k]):
+                    g, hh = divmod(h, HEADS_PER_PASS)
+                    nc.scalar.activation(
+                        out=a_sb[i][:, g, :, hh, :],
+                        in_=hs_ps[i][k][:, slot, 0:D].rearrange("p (u w) -> p u w", u=2),
+                        func=ACT.Copy,
+                        scale=r_den[i][:, 3 * k + slot : 3 * k + slot + 1],
+                    )
+            nc.vector.tensor_tensor(
+                out=a_sb[i][:, :, :, HEADS_PER_PASS - 1, :],
+                in0=hs_ps[i][2][:, 0:2, 0:D].rearrange("p g (u w) -> p g u w", u=2),
+                in1=r_den[i][:, 6:8].unsqueeze(2).unsqueeze(3).to_broadcast([P, 2, 2, D // 2]),
+                op=ALU.mult,
+            )
+
+        def transpose_a(i):
+            a_ps = ps_one.tile([P, PASSES, 2, P], F32, name="a_ps", tag="a")
+            for g in range(PASSES):
+                for u in range(2):
+                    nc.tensor.transpose(
+                        out=a_ps[:, g, u, :],
+                        in_=a_sb[i][:, g, u, :, :].rearrange("p h w -> p (h w)").bitcast(F32),
+                        identity=ident_f32[:],
+                    )
+            grouped[i] = work.tile([P, PASSES, P, PACK], BF16, name="grouped", align_bytes=64)
+            nc.scalar.copy(
+                out=grouped[i][:]
+                .rearrange("p g s t -> p (g s t)")
+                .bitcast(F32)
+                .rearrange("p (g s u) -> p g s u", g=PASSES, u=2),
+                in_=a_ps[:].rearrange("p g u s -> p g s u"),
+            )
+
+        def quantise(i):
+            codes[i] = work.tile([P, PASSES * P], U32, name="codes", align_bytes=64)
+            a_scales[i] = work.tile([P, PASSES * P], U8, name="a_scales", align_bytes=64)
+            nc.vector.quantize_mx(
+                out=codes[i][:].bitcast(FP8X4),
+                scales=a_scales[i][:],
+                in_=grouped[i][:].rearrange("p g s t -> p (g s t)"),
+            )
+
+        def project(i):
+            out_ps[i] = []
+            for nh in range(N_HALVES):
+                acc = ps_one.tile([P, N_MX], F32, name="acc", tag="o%d" % nh)
+                for g in range(PASSES):
+                    tokens = slice(g * P, (g + 1) * P)
+                    nc.tensor.matmul_mx(
+                        out=acc[:],
+                        lhsT=codes[i][:, tokens].bitcast(FP8X4),
+                        lhsT_scale=a_scales[i][:, tokens],
+                        rhs=w_words[:, g, nh * N_MX * PACK : (nh + 1) * N_MX * PACK].bitcast(FP8X4),
+                        rhs_scale=w_scales[:, g, nh * N_MX : (nh + 1) * N_MX],
+                        start=(g == 0),
+                        stop=(g == PASSES - 1),
+                    )
+                out_ps[i].append(acc)
+
+        def add_bias_and_store(i):
+            b, r = divmod(i, ROWS)
+            out_sb = work.tile([P, C], F32, name="out_sb")
+            for nh in range(N_HALVES):
+                cols = slice(nh * N_MX, (nh + 1) * N_MX)
+                nc.vector.tensor_tensor(out=out_sb[:, cols], in0=out_ps[i][nh][:], in1=bias_sb[:, cols], op=ALU.add)
+            nc.sync.dma_start(out=out[b].rearrange("(p r) c -> r p c", r=ROWS)[r], in_=out_sb[:])
+
+        transpose_vk(0)
+        transpose_q(0)
+        transpose_q(1)
+        for i in range(TILES + 2):
+            if i < TILES:
+                read_out(i)
+            if i >= 2:
+                project(i - 2)
+            if i < TILES:
+                normalise(i)
+            if 1 <= i <= TILES:
+                quantise(i - 1)
+            if i >= 2:
+                add_bias_and_store(i - 2)
+            if i + 2 < TILES:
+                if (i + 2) % ROWS == 0:
+                    transpose_vk((i + 2) // ROWS)
+                transpose_q(i + 2)
+            if i < TILES:
+                transpose_a(i)

@@ -27,6 +27,8 @@ TILES = B * ROWS
 VK_PITCH = 136
 
 BANK_HEADS = ((0, 1, 2), (4, 5, 6), (3, 7))
+SCALAR_BANKS = (0, 2)
+VECTOR_BANK = 1
 
 FLOPS = 2 * B * S * (H * D) * C + 2 * B * H * S * D * D + 2 * B * H * S * D
 
@@ -61,10 +63,10 @@ def tile_lineartransformerblock_pc_kernel(tc, q_feat, vk, k_sum, Wo_words, Wo_sc
         def load_vk(b):
             nc.sync.dma_start(out=vk_sb[b][:], in_=vk[b].rearrange("h n d -> n h d"))
 
-        load_q(0, 0)
-        load_vk(0)
-        load_q(0, 1)
         nc.sync.dma_start(out=ks_sb[0 : B * H, :], in_=k_sum.rearrange("b h d -> (b h) d"))
+        load_vk(0)
+        load_q(0, 0)
+        load_q(0, 1)
         nc.sync.dma_start(out=bias_row[0:1, :], in_=bo.rearrange("(o c) -> o c", o=1))
         for quad in range(4):
             nc.sync.dma_start(
@@ -94,11 +96,17 @@ def tile_lineartransformerblock_pc_kernel(tc, q_feat, vk, k_sum, Wo_words, Wo_sc
         )
 
         bias_sb = keep.tile([P, C], F32, name="bias_sb")
-        for nh in range(N_HALVES):
-            cols = slice(nh * N_MX, (nh + 1) * N_MX)
-            bias_ps = ps_one.tile([P, N_MX], F32, name="bias_ps", tag="o%d" % nh)
-            nc.tensor.matmul(out=bias_ps[:], lhsT=ones_bf[:], rhs=bias_row[:, cols], start=True, stop=True)
-            nc.vector.tensor_copy(out=bias_sb[:, cols], in_=bias_ps[:])
+
+        def spread_bias():
+            for nh in range(N_HALVES):
+                cols = slice(nh * N_MX, (nh + 1) * N_MX)
+                bias_ps = ps_one.tile([P, N_MX], F32, name="bias_ps", tag="o%d" % nh)
+                nc.tensor.matmul(out=bias_ps[:], lhsT=ones_bf[:], rhs=bias_row[:, cols], start=True, stop=True)
+                nc.vector.tensor_copy(out=bias_sb[:, cols], in_=bias_ps[:])
+
+        warm = keep.tile([P, 1], F32, name="warm")
+        nc.vector.memset(warm[:], 0.0)
+        nc.scalar.activation(out=warm[:], in_=warm[:], func=ACT.Copy)
 
         vk_t = keep.tile([P, B * H, VK_PITCH], BF16, name="vk_t")
         ks_ps = ps_t.tile([P, H, P], BF16, name="ks_ps", tag="t")
@@ -113,6 +121,7 @@ def tile_lineartransformerblock_pc_kernel(tc, q_feat, vk, k_sum, Wo_words, Wo_sc
 
         q_t = {}
         hs_ps = {}
+        den_sb = {}
         r_den = {}
         a_sb = {}
         grouped = {}
@@ -147,12 +156,13 @@ def tile_lineartransformerblock_pc_kernel(tc, q_feat, vk, k_sum, Wo_words, Wo_sc
                 nc.vector.tensor_scalar_add(
                     out=den[:, 3 * k : 3 * k + len(heads)], in0=hs_ps[i][k][:, 0 : len(heads), D], scalar1=EPS
                 )
-            r_den[i] = work.tile([P, H], F32, name="r_den")
-            nc.vector.reciprocal(out=r_den[i][:], in_=den[:])
+            den_sb[i] = den
 
         def normalise(i):
+            r_den[i] = work.tile([P, H], F32, name="r_den")
+            nc.vector.reciprocal(out=r_den[i][:], in_=den_sb[i][:])
             a_sb[i] = work.tile([P, PASSES, 2, HEADS_PER_PASS, D // 2], BF16, name="a_sb")
-            for k in range(2):
+            for k in SCALAR_BANKS:
                 for slot, h in enumerate(BANK_HEADS[k]):
                     g, hh = divmod(h, HEADS_PER_PASS)
                     nc.scalar.activation(
@@ -162,9 +172,9 @@ def tile_lineartransformerblock_pc_kernel(tc, q_feat, vk, k_sum, Wo_words, Wo_sc
                         scale=r_den[i][:, 3 * k + slot : 3 * k + slot + 1],
                     )
             nc.vector.tensor_tensor(
-                out=a_sb[i][:, :, :, HEADS_PER_PASS - 1, :],
-                in0=hs_ps[i][2][:, 0:2, 0:D].rearrange("p g (u w) -> p g u w", u=2),
-                in1=r_den[i][:, 6:8].unsqueeze(2).unsqueeze(3).to_broadcast([P, 2, 2, D // 2]),
+                out=a_sb[i][:, 1, :, 0:3, :].rearrange("p u h w -> p h u w"),
+                in0=hs_ps[i][VECTOR_BANK][:, :, 0:D].rearrange("p h (u w) -> p h u w", u=2),
+                in1=r_den[i][:, 3:6].unsqueeze(2).unsqueeze(3).to_broadcast([P, 3, 2, D // 2]),
                 op=ALU.mult,
             )
 
@@ -223,20 +233,22 @@ def tile_lineartransformerblock_pc_kernel(tc, q_feat, vk, k_sum, Wo_words, Wo_sc
         transpose_vk(0)
         transpose_q(0)
         transpose_q(1)
-        for i in range(TILES + 2):
+        for i in range(TILES + 3):
             if i < TILES:
                 read_out(i)
-            if i >= 2:
-                project(i - 2)
+            if i == 0:
+                spread_bias()
+            if i >= 3:
+                project(i - 3)
+            if 2 <= i < TILES + 2:
+                quantise(i - 2)
             if i < TILES:
                 normalise(i)
-            if 1 <= i <= TILES:
-                quantise(i - 1)
-            if i >= 2:
-                add_bias_and_store(i - 2)
+            if i >= 3:
+                add_bias_and_store(i - 3)
             if i + 2 < TILES:
                 if (i + 2) % ROWS == 0:
                     transpose_vk((i + 2) // ROWS)
                 transpose_q(i + 2)
-            if i < TILES:
-                transpose_a(i)
+            if 1 <= i < TILES + 1:
+                transpose_a(i - 1)

@@ -97,12 +97,19 @@ def tile_lineartransformerblock_pc_kernel(tc, q_feat, vk, k_sum, Wo_words, Wo_sc
 
         bias_sb = keep.tile([P, C], F32, name="bias_sb")
 
+        bias_ps = []
+
         def spread_bias():
             for nh in range(N_HALVES):
-                cols = slice(nh * N_MX, (nh + 1) * N_MX)
-                bias_ps = ps_one.tile([P, N_MX], F32, name="bias_ps", tag="o%d" % nh)
-                nc.tensor.matmul(out=bias_ps[:], lhsT=ones_bf[:], rhs=bias_row[:, cols], start=True, stop=True)
-                nc.vector.tensor_copy(out=bias_sb[:, cols], in_=bias_ps[:])
+                bank = ps_one.tile([P, N_MX], F32, name="bias_ps", tag="o%d" % nh)
+                nc.tensor.matmul(
+                    out=bank[:], lhsT=ones_bf[:], rhs=bias_row[:, nh * N_MX : (nh + 1) * N_MX], start=True, stop=True
+                )
+                bias_ps.append(bank)
+
+        def keep_bias():
+            for nh in range(N_HALVES):
+                nc.vector.tensor_copy(out=bias_sb[:, nh * N_MX : (nh + 1) * N_MX], in_=bias_ps[nh][:])
 
         warm = keep.tile([P, 1], F32, name="warm")
         nc.vector.memset(warm[:], 0.0)
@@ -111,13 +118,13 @@ def tile_lineartransformerblock_pc_kernel(tc, q_feat, vk, k_sum, Wo_words, Wo_sc
         vk_t = keep.tile([P, B * H, VK_PITCH], BF16, name="vk_t")
         ks_ps = ps_t.tile([P, H, P], BF16, name="ks_ps", tag="t")
         nc.tensor.transpose(out=ks_ps[:, 0, :], in_=ks_sb[:], identity=ident_bf[:])
-        nc.scalar.copy(out=vk_t[:, :, D], in_=ks_ps[:, 0, 0 : B * H])
+        nc.vector.tensor_copy(out=vk_t[:, :, D], in_=ks_ps[:, 0, 0 : B * H])
 
         def transpose_vk(b):
             vk_ps = ps_t.tile([P, H, P], BF16, name="vk_ps", tag="t")
             for h in range(H):
                 nc.tensor.transpose(out=vk_ps[:, h, :], in_=vk_sb[b][:, h, :], identity=order_n[:])
-            nc.scalar.copy(out=vk_t[:, b * H : (b + 1) * H, 0:D], in_=vk_ps[:])
+            nc.vector.tensor_copy(out=vk_t[:, b * H : (b + 1) * H, 0:D], in_=vk_ps[:])
 
         q_t = {}
         hs_ps = {}
@@ -128,6 +135,7 @@ def tile_lineartransformerblock_pc_kernel(tc, q_feat, vk, k_sum, Wo_words, Wo_sc
         codes = {}
         a_scales = {}
         out_ps = {}
+        out_sb = {}
 
         def transpose_q(i):
             b, r = divmod(i, ROWS)
@@ -158,9 +166,11 @@ def tile_lineartransformerblock_pc_kernel(tc, q_feat, vk, k_sum, Wo_words, Wo_sc
                 )
             den_sb[i] = den
 
-        def normalise(i):
+        def reciprocal(i):
             r_den[i] = work.tile([P, H], F32, name="r_den")
             nc.vector.reciprocal(out=r_den[i][:], in_=den_sb[i][:])
+
+        def normalise(i):
             a_sb[i] = work.tile([P, PASSES, 2, HEADS_PER_PASS, D // 2], BF16, name="a_sb")
             for k in SCALAR_BANKS:
                 for slot, h in enumerate(BANK_HEADS[k]):
@@ -222,13 +232,15 @@ def tile_lineartransformerblock_pc_kernel(tc, q_feat, vk, k_sum, Wo_words, Wo_sc
                     )
                 out_ps[i].append(acc)
 
-        def add_bias_and_store(i):
+        def add_bias(i, nh):
+            if nh == 0:
+                out_sb[i] = work.tile([P, C], F32, name="out_sb")
+            cols = slice(nh * N_MX, (nh + 1) * N_MX)
+            nc.vector.tensor_tensor(out=out_sb[i][:, cols], in0=out_ps[i][nh][:], in1=bias_sb[:, cols], op=ALU.add)
+
+        def store(i):
             b, r = divmod(i, ROWS)
-            out_sb = work.tile([P, C], F32, name="out_sb")
-            for nh in range(N_HALVES):
-                cols = slice(nh * N_MX, (nh + 1) * N_MX)
-                nc.vector.tensor_tensor(out=out_sb[:, cols], in0=out_ps[i][nh][:], in1=bias_sb[:, cols], op=ALU.add)
-            nc.sync.dma_start(out=out[b].rearrange("(p r) c -> r p c", r=ROWS)[r], in_=out_sb[:])
+            nc.sync.dma_start(out=out[b].rearrange("(p r) c -> r p c", r=ROWS)[r], in_=out_sb[i][:])
 
         transpose_vk(0)
         transpose_q(0)
@@ -240,12 +252,19 @@ def tile_lineartransformerblock_pc_kernel(tc, q_feat, vk, k_sum, Wo_words, Wo_sc
                 spread_bias()
             if i >= 3:
                 project(i - 3)
-            if 2 <= i < TILES + 2:
-                quantise(i - 2)
+            if i < TILES:
+                reciprocal(i)
+            if i >= 3:
+                add_bias(i - 3, 0)
             if i < TILES:
                 normalise(i)
+            if i == 0:
+                keep_bias()
+            if 2 <= i < TILES + 2:
+                quantise(i - 2)
             if i >= 3:
-                add_bias_and_store(i - 3)
+                add_bias(i - 3, 1)
+                store(i - 3)
             if i + 2 < TILES:
                 if (i + 2) % ROWS == 0:
                     transpose_vk((i + 2) // ROWS)

@@ -37,7 +37,7 @@ def tile_lineartransformerblock_pc_kernel(tc, q_feat, vk, k_sum, Wo_words, Wo_sc
     nc = tc.nc
     with ExitStack() as ctx:
         keep = ctx.enter_context(tc.tile_pool(name="keep", bufs=1))
-        work = ctx.enter_context(tc.tile_pool(name="work", bufs=3))
+        work = ctx.enter_context(tc.tile_pool(name="work", bufs=4))
         ps_t = ctx.enter_context(tc.psum_pool(name="ps_t", bufs=2))
         ps_one = ctx.enter_context(tc.psum_pool(name="ps_one", bufs=1))
         ctx.enter_context(tc.manual_schedule())
@@ -53,6 +53,11 @@ def tile_lineartransformerblock_pc_kernel(tc, q_feat, vk, k_sum, Wo_words, Wo_sc
         nc.vector.memset(bias_row[:], 0.0)
         nc.vector.memset(w_scales[:].rearrange("p g n -> p (g n)").bitcast(I32), 0)
 
+        def load_q_tile(b, r):
+            nc.sync.dma_start(
+                out=q_sb[b][:, :, r, :], in_=q_feat[b].rearrange("h (p r) d -> r p h d", r=ROWS)[r]
+            )
+
         def load_q(b, half):
             heads = slice(half * HEADS_PER_PASS, (half + 1) * HEADS_PER_PASS)
             nc.sync.dma_start(
@@ -63,11 +68,18 @@ def tile_lineartransformerblock_pc_kernel(tc, q_feat, vk, k_sum, Wo_words, Wo_sc
         def load_vk(b):
             nc.sync.dma_start(out=vk_sb[b][:], in_=vk[b].rearrange("h n d -> n h d"))
 
-        nc.sync.dma_start(out=ks_sb[0 : B * H, :], in_=k_sum.rearrange("b h d -> (b h) d"))
+        def load_batch(b):
+            load_vk(b)
+            load_q(b, 0)
+            load_q(b, 1)
+
+        load_q_tile(0, 0)
         load_vk(0)
-        load_q(0, 0)
-        load_q(0, 1)
+        nc.sync.dma_start(out=ks_sb[0 : B * H, :], in_=k_sum.rearrange("b h d -> (b h) d"))
         nc.sync.dma_start(out=bias_row[0:1, :], in_=bo.rearrange("(o c) -> o c", o=1))
+        for r in range(1, ROWS):
+            load_q_tile(0, r)
+        load_batch(1)
         for quad in range(4):
             nc.sync.dma_start(
                 out=w_scales[32 * quad : 32 * quad + 4, :, :].bitcast(I32),
@@ -78,10 +90,8 @@ def tile_lineartransformerblock_pc_kernel(tc, q_feat, vk, k_sum, Wo_words, Wo_sc
                 out=w_words[:, g, :].bitcast(I32),
                 in_=Wo_words[g].rearrange("p n t -> p (n t)").bitcast(I32),
             )
-        for b in range(1, B):
-            load_vk(b)
-            load_q(b, 0)
-            load_q(b, 1)
+        load_batch(2)
+        load_batch(3)
 
         ident_bf = keep.tile([P, P], BF16, name="ident_bf")
         make_identity(nc, ident_bf[:])
@@ -116,9 +126,11 @@ def tile_lineartransformerblock_pc_kernel(tc, q_feat, vk, k_sum, Wo_words, Wo_sc
         nc.scalar.activation(out=warm[:], in_=warm[:], func=ACT.Copy)
 
         vk_t = keep.tile([P, B * H, VK_PITCH], BF16, name="vk_t")
-        ks_ps = ps_t.tile([P, H, P], BF16, name="ks_ps", tag="t")
-        nc.tensor.transpose(out=ks_ps[:, 0, :], in_=ks_sb[:], identity=ident_bf[:])
-        nc.vector.tensor_copy(out=vk_t[:, :, D], in_=ks_ps[:, 0, 0 : B * H])
+
+        def transpose_k_sum():
+            ks_ps = ps_t.tile([P, H, P], BF16, name="ks_ps", tag="t")
+            nc.tensor.transpose(out=ks_ps[:, 0, :], in_=ks_sb[:], identity=ident_bf[:])
+            nc.vector.tensor_copy(out=vk_t[:, :, D], in_=ks_ps[:, 0, 0 : B * H])
 
         def transpose_vk(b):
             vk_ps = ps_t.tile([P, H, P], BF16, name="vk_ps", tag="t")
@@ -232,39 +244,38 @@ def tile_lineartransformerblock_pc_kernel(tc, q_feat, vk, k_sum, Wo_words, Wo_sc
                     )
                 out_ps[i].append(acc)
 
-        def add_bias(i, nh):
+        def add_bias_and_store(i, nh):
             if nh == 0:
                 out_sb[i] = work.tile([P, C], F32, name="out_sb")
             cols = slice(nh * N_MX, (nh + 1) * N_MX)
             nc.vector.tensor_tensor(out=out_sb[i][:, cols], in0=out_ps[i][nh][:], in1=bias_sb[:, cols], op=ALU.add)
 
-        def store(i):
             b, r = divmod(i, ROWS)
-            nc.sync.dma_start(out=out[b].rearrange("(p r) c -> r p c", r=ROWS)[r], in_=out_sb[i][:])
+            nc.sync.dma_start(out=out[b].rearrange("(p r) c -> r p c", r=ROWS)[r][:, cols], in_=out_sb[i][:, cols])
 
-        transpose_vk(0)
         transpose_q(0)
+        transpose_vk(0)
+        transpose_k_sum()
         transpose_q(1)
-        for i in range(TILES + 3):
+        for i in range(TILES + 4):
             if i < TILES:
                 read_out(i)
-            if i == 0:
+            if i == 1:
                 spread_bias()
-            if i >= 3:
-                project(i - 3)
+            if i >= 4:
+                project(i - 4)
+            if 3 <= i < TILES + 3:
+                quantise(i - 3)
             if i < TILES:
                 reciprocal(i)
-            if i >= 3:
-                add_bias(i - 3, 0)
+            if i >= 4:
+                add_bias_and_store(i - 4, 0)
             if i < TILES:
                 normalise(i)
-            if i == 0:
+            if i == 1:
                 keep_bias()
-            if 2 <= i < TILES + 2:
-                quantise(i - 2)
-            if i >= 3:
-                add_bias(i - 3, 1)
-                store(i - 3)
+            if i >= 4:
+                add_bias_and_store(i - 4, 1)
             if i + 2 < TILES:
                 if (i + 2) % ROWS == 0:
                     transpose_vk((i + 2) // ROWS)

@@ -25,12 +25,29 @@ N_HALVES = C // N_MX
 ROWS = S // P
 TILES = B * ROWS
 VK_PITCH = 136
-
 BANK_HEADS = ((0, 1, 2), (4, 5, 6), (3, 7))
-SCALAR_BANKS = (0, 2)
-VECTOR_BANK = 1
 
 FLOPS = 2 * B * S * (H * D) * C + 2 * B * H * S * D * D + 2 * B * H * S * D
+
+HS_BUFS = 3
+LP = 4
+WARM0 = 0
+WARM_FILL = ()
+SPLIT_RECIP = 1
+LEAD = (2, 2, 2, 2)
+LEAD_STEADY = 2
+QCOPY_V = 0
+FILL_V5 = 0
+ORDER = 0
+DRAIN_BANKS = 1
+PRO = 2
+WARM1 = 0
+TEMPLATE = (("R", 0), ("den", 0), ("bias", 1), ("P", 4), ("qz", 3), ("rec", 0), ("b0", 4), ("na", 0), ("nA0", 0), ("n2", 0), ("nV1", 0), ("kbias", 1), ("b1", 4), ("Q", 0), ("TA", 1), ("cA", 1))
+LOADS = "q00 v0 ks bias q01 q02 q03 v1 h10 h11 ws ww v2 h20 h21 v3 h30 h31"
+HEAD_BANKS = 1
+XTRA = ()
+QV_LO = 2
+QV_HI = 6
 
 
 def tile_lineartransformerblock_pc_kernel(tc, q_feat, vk, k_sum, Wo_words, Wo_scales, bo, out):
@@ -48,9 +65,12 @@ def tile_lineartransformerblock_pc_kernel(tc, q_feat, vk, k_sum, Wo_words, Wo_sc
         bias_row = keep.tile([P, C], BF16, name="bias_row")
         w_words = keep.tile([P, PASSES, C * PACK], U8, name="w_words", align_bytes=64)
         w_scales = keep.tile([P, PASSES, C], U8, name="w_scales", align_bytes=64)
-
-        nc.vector.memset(ks_sb[:], 0.0)
+        ones_bf = keep.tile([P, P], BF16, name="ones_bf")
+        zeros = keep.tile([P, N_MX], BF16, name="zeros")
+        nc.vector.memset(zeros[:], 0.0)
+        nc.vector.memset(ones_bf[:], 1.0)
         nc.vector.memset(bias_row[:], 0.0)
+        nc.vector.memset(ks_sb[:], 0.0)
         nc.vector.memset(w_scales[:].rearrange("p g n -> p (g n)").bitcast(I32), 0)
 
         def load_q_tile(b, r):
@@ -73,40 +93,51 @@ def tile_lineartransformerblock_pc_kernel(tc, q_feat, vk, k_sum, Wo_words, Wo_sc
             load_q(b, 0)
             load_q(b, 1)
 
-        load_q_tile(0, 0)
-        load_vk(0)
-        nc.sync.dma_start(out=ks_sb[0 : B * H, :], in_=k_sum.rearrange("b h d -> (b h) d"))
-        nc.sync.dma_start(out=bias_row[0:1, :], in_=bo.rearrange("(o c) -> o c", o=1))
-        for r in range(1, ROWS):
-            load_q_tile(0, r)
-        load_batch(1)
-        for quad in range(4):
-            nc.sync.dma_start(
-                out=w_scales[32 * quad : 32 * quad + 4, :, :].bitcast(I32),
-                in_=Wo_scales[:, 4 * quad : 4 * quad + 4, :].rearrange("g r n -> r g n").bitcast(I32),
-            )
-        for g in range(PASSES):
-            nc.sync.dma_start(
-                out=w_words[:, g, :].bitcast(I32),
-                in_=Wo_words[g].rearrange("p n t -> p (n t)").bitcast(I32),
-            )
-        load_batch(2)
-        load_batch(3)
+        def load_ws():
+            for quad in range(4):
+                nc.sync.dma_start(
+                    out=w_scales[32 * quad : 32 * quad + 4, :, :].bitcast(I32),
+                    in_=Wo_scales[:, 4 * quad : 4 * quad + 4, :].rearrange("g r n -> r g n").bitcast(I32),
+                )
+
+        def load_ww():
+            for g in range(PASSES):
+                nc.sync.dma_start(
+                    out=w_words[:, g, :].bitcast(I32),
+                    in_=Wo_words[g].rearrange("p n t -> p (n t)").bitcast(I32),
+                )
+
+        for tok in LOADS.split():
+            if tok[0] == "q":
+                load_q_tile(int(tok[1]), int(tok[2]))
+            elif tok[0] == "v":
+                load_vk(int(tok[1]))
+            elif tok[0] == "h":
+                load_q(int(tok[1]), int(tok[2]))
+            elif tok == "ks":
+                nc.sync.dma_start(out=ks_sb[0 : B * H, :], in_=k_sum.rearrange("b h d -> (b h) d"))
+            elif tok == "bias":
+                nc.sync.dma_start(out=bias_row[0:1, :], in_=bo.rearrange("(o c) -> o c", o=1))
+            elif tok == "ws":
+                load_ws()
+            elif tok == "ww":
+                load_ww()
+
+        def warm_up(n):
+            for k in range(n):
+                junk = ps_one.tile([P, N_MX], F32, name="junk", tag="o%d" % (k % 2))
+                nc.tensor.matmul(out=junk[:], lhsT=zeros[:, 0:P], rhs=zeros[:], start=True, stop=True)
 
         ident_bf = keep.tile([P, P], BF16, name="ident_bf")
         make_identity(nc, ident_bf[:])
         ident_f32 = keep.tile([P, P], F32, name="ident_f32")
         make_identity(nc, ident_f32[:])
-        ones_bf = keep.tile([P, P], BF16, name="ones_bf")
-        nc.vector.memset(ones_bf[:], 1.0)
         order_n = keep.tile([P, P], BF16, name="order_n")
         nc.vector.tensor_copy(
             out=order_n[:].rearrange("p (u j e) -> p u j e", u=2, j=32, e=2),
             in_=ident_bf[:].rearrange("p (j u e) -> p u j e", j=32, u=2, e=2),
         )
-
         bias_sb = keep.tile([P, C], F32, name="bias_sb")
-
         bias_ps = []
 
         def spread_bias():
@@ -128,17 +159,25 @@ def tile_lineartransformerblock_pc_kernel(tc, q_feat, vk, k_sum, Wo_words, Wo_sc
         vk_t = keep.tile([P, B * H, VK_PITCH], BF16, name="vk_t")
 
         def transpose_k_sum():
-            ks_ps = ps_t.tile([P, H, P], BF16, name="ks_ps", tag="t")
+            if HEAD_BANKS:
+                ks_ps = ps_one.tile([P, H, P], BF16, name="ks_ps", tag="o0")
+            else:
+                ks_ps = ps_t.tile([P, H, P], BF16, name="ks_ps", tag="t")
             nc.tensor.transpose(out=ks_ps[:, 0, :], in_=ks_sb[:], identity=ident_bf[:])
             nc.vector.tensor_copy(out=vk_t[:, :, D], in_=ks_ps[:, 0, 0 : B * H])
 
         def transpose_vk(b):
-            vk_ps = ps_t.tile([P, H, P], BF16, name="vk_ps", tag="t")
+            if HEAD_BANKS and b == 0:
+                vk_ps = ps_one.tile([P, H, P], BF16, name="vk_ps", tag="a")
+            else:
+                vk_ps = ps_t.tile([P, H, P], BF16, name="vk_ps", tag="t")
             for h in range(H):
                 nc.tensor.transpose(out=vk_ps[:, h, :], in_=vk_sb[b][:, h, :], identity=order_n[:])
             nc.vector.tensor_copy(out=vk_t[:, b * H : (b + 1) * H, 0:D], in_=vk_ps[:])
 
         q_t = {}
+        q_pss = {}
+        a_pss = {}
         hs_ps = {}
         den_sb = {}
         r_den = {}
@@ -149,20 +188,32 @@ def tile_lineartransformerblock_pc_kernel(tc, q_feat, vk, k_sum, Wo_words, Wo_sc
         out_ps = {}
         out_sb = {}
 
-        def transpose_q(i):
+        def transpose_q(i, tag=None):
             b, r = divmod(i, ROWS)
-            q_ps = ps_t.tile([P, H, P], BF16, name="q_ps", tag="t")
+            if tag:
+                q_ps = ps_one.tile([P, H, P], BF16, name="q_ps", tag=tag)
+            else:
+                q_ps = ps_t.tile([P, H, P], BF16, name="q_ps", tag="t")
             for h in range(H):
                 nc.tensor.transpose(out=q_ps[:, h, :], in_=q_sb[b][:, h, r, :], identity=ident_bf[:])
-            q_t[i] = work.tile([P, H, P], BF16, name="q_t")
-            nc.scalar.copy(out=q_t[i][:], in_=q_ps[:])
+            q_pss[i] = q_ps
+
+        def copy_q(i, on_vector=False):
+            q_ps = q_pss[i]
+            q_t[i] = work.tile([P, H, P], BF16, name="q_t", bufs=TILES)
+            if on_vector or (QCOPY_V and i % QCOPY_V == QCOPY_V - 1) or QV_LO <= i < QV_HI:
+                nc.vector.tensor_copy(out=q_t[i][:], in_=q_ps[:])
+            else:
+                nc.scalar.copy(out=q_t[i][:], in_=q_ps[:])
 
         def read_out(i):
             b = i // ROWS
             hs_ps[i] = []
-            den = work.tile([P, H], F32, name="den")
             for k, heads in enumerate(BANK_HEADS):
-                bank = ps_one.tile([P, 3, D + 1], F32, name="hs_ps", tag="hs%d" % k)
+                if HS_BUFS == 4:
+                    bank = ps_one.tile([P, 3, D + 1], F32, name="hs_ps", tag="hs", bufs=4)
+                else:
+                    bank = ps_one.tile([P, 3, D + 1], F32, name="hs_ps", tag="hs%d" % k)
                 for slot, h in enumerate(heads):
                     nc.tensor.matmul(
                         out=bank[:, slot, :],
@@ -172,6 +223,9 @@ def tile_lineartransformerblock_pc_kernel(tc, q_feat, vk, k_sum, Wo_words, Wo_sc
                         stop=True,
                     )
                 hs_ps[i].append(bank)
+
+        def den_add(i):
+            den = work.tile([P, H], F32, name="den")
             for k, heads in enumerate(BANK_HEADS):
                 nc.vector.tensor_scalar_add(
                     out=den[:, 3 * k : 3 * k + len(heads)], in0=hs_ps[i][k][:, 0 : len(heads), D], scalar1=EPS
@@ -180,28 +234,47 @@ def tile_lineartransformerblock_pc_kernel(tc, q_feat, vk, k_sum, Wo_words, Wo_sc
 
         def reciprocal(i):
             r_den[i] = work.tile([P, H], F32, name="r_den")
-            nc.vector.reciprocal(out=r_den[i][:], in_=den_sb[i][:])
+            if SPLIT_RECIP:
+                for k, heads in enumerate(BANK_HEADS):
+                    cols = slice(3 * k, 3 * k + len(heads))
+                    nc.vector.reciprocal(out=r_den[i][:, cols], in_=den_sb[i][:, cols])
+            else:
+                nc.vector.reciprocal(out=r_den[i][:], in_=den_sb[i][:])
 
-        def normalise(i):
+        def norm_scalar(i, k):
+            for slot, h in enumerate(BANK_HEADS[k]):
+                g, hh = divmod(h, HEADS_PER_PASS)
+                nc.scalar.activation(
+                    out=a_sb[i][:, g, :, hh, :],
+                    in_=hs_ps[i][k][:, slot, 0:D].rearrange("p (u w) -> p u w", u=2),
+                    func=ACT.Copy,
+                    scale=r_den[i][:, 3 * k + slot : 3 * k + slot + 1],
+                )
+
+        def norm_vector(i, k):
+            if k == 1:
+                nc.vector.tensor_tensor(
+                    out=a_sb[i][:, 1, :, 0:3, :].rearrange("p u h w -> p h u w"),
+                    in0=hs_ps[i][1][:, :, 0:D].rearrange("p h (u w) -> p h u w", u=2),
+                    in1=r_den[i][:, 3:6].unsqueeze(2).unsqueeze(3).to_broadcast([P, 3, 2, D // 2]),
+                    op=ALU.mult,
+                )
+            else:
+                nc.vector.tensor_tensor(
+                    out=a_sb[i][:, :, :, 3, :],
+                    in0=hs_ps[i][2][:, 0:2, 0:D].rearrange("p h (u w) -> p h u w", u=2),
+                    in1=r_den[i][:, 6:8].unsqueeze(2).unsqueeze(3).to_broadcast([P, 2, 2, D // 2]),
+                    op=ALU.mult,
+                )
+
+        def new_a(i):
             a_sb[i] = work.tile([P, PASSES, 2, HEADS_PER_PASS, D // 2], BF16, name="a_sb")
-            for k in SCALAR_BANKS:
-                for slot, h in enumerate(BANK_HEADS[k]):
-                    g, hh = divmod(h, HEADS_PER_PASS)
-                    nc.scalar.activation(
-                        out=a_sb[i][:, g, :, hh, :],
-                        in_=hs_ps[i][k][:, slot, 0:D].rearrange("p (u w) -> p u w", u=2),
-                        func=ACT.Copy,
-                        scale=r_den[i][:, 3 * k + slot : 3 * k + slot + 1],
-                    )
-            nc.vector.tensor_tensor(
-                out=a_sb[i][:, 1, :, 0:3, :].rearrange("p u h w -> p h u w"),
-                in0=hs_ps[i][VECTOR_BANK][:, :, 0:D].rearrange("p h (u w) -> p h u w", u=2),
-                in1=r_den[i][:, 3:6].unsqueeze(2).unsqueeze(3).to_broadcast([P, 3, 2, D // 2]),
-                op=ALU.mult,
-            )
 
         def transpose_a(i):
-            a_ps = ps_one.tile([P, PASSES, 2, P], F32, name="a_ps", tag="a")
+            if HS_BUFS == 4:
+                a_ps = ps_t.tile([P, PASSES, 2, P], F32, name="a_ps", tag="t")
+            else:
+                a_ps = ps_one.tile([P, PASSES, 2, P], F32, name="a_ps", tag="a")
             for g in range(PASSES):
                 for u in range(2):
                     nc.tensor.transpose(
@@ -209,6 +282,10 @@ def tile_lineartransformerblock_pc_kernel(tc, q_feat, vk, k_sum, Wo_words, Wo_sc
                         in_=a_sb[i][:, g, u, :, :].rearrange("p h w -> p (h w)").bitcast(F32),
                         identity=ident_f32[:],
                     )
+            a_pss[i] = a_ps
+
+        def copy_a(i):
+            a_ps = a_pss[i]
             grouped[i] = work.tile([P, PASSES, P, PACK], BF16, name="grouped", align_bytes=64)
             nc.scalar.copy(
                 out=grouped[i][:]
@@ -227,10 +304,14 @@ def tile_lineartransformerblock_pc_kernel(tc, q_feat, vk, k_sum, Wo_words, Wo_sc
                 in_=grouped[i][:].rearrange("p g s t -> p (g s t)"),
             )
 
-        def project(i):
-            out_ps[i] = []
-            for nh in range(N_HALVES):
-                acc = ps_one.tile([P, N_MX], F32, name="acc", tag="o%d" % nh)
+        def project(i, halves=(0, 1)):
+            if 0 in halves:
+                out_ps[i] = []
+            for nh in halves:
+                if DRAIN_BANKS and i == TILES - 2:
+                    acc = ps_one.tile([P, N_MX], F32, name="acc", tag="hs%d" % nh)
+                else:
+                    acc = ps_one.tile([P, N_MX], F32, name="acc", tag="o%d" % nh)
                 for g in range(PASSES):
                     tokens = slice(g * P, (g + 1) * P)
                     nc.tensor.matmul_mx(
@@ -249,36 +330,57 @@ def tile_lineartransformerblock_pc_kernel(tc, q_feat, vk, k_sum, Wo_words, Wo_sc
                 out_sb[i] = work.tile([P, C], F32, name="out_sb")
             cols = slice(nh * N_MX, (nh + 1) * N_MX)
             nc.vector.tensor_tensor(out=out_sb[i][:, cols], in0=out_ps[i][nh][:], in1=bias_sb[:, cols], op=ALU.add)
-
             b, r = divmod(i, ROWS)
             nc.sync.dma_start(out=out[b].rearrange("(p r) c -> r p c", r=ROWS)[r][:, cols], in_=out_sb[i][:, cols])
 
-        transpose_q(0)
-        transpose_vk(0)
-        transpose_k_sum()
-        transpose_q(1)
-        for i in range(TILES + 4):
-            if i < TILES:
-                read_out(i)
-            if i == 1:
-                spread_bias()
-            if i >= 4:
-                project(i - 4)
-            if 3 <= i < TILES + 3:
-                quantise(i - 3)
-            if i < TILES:
-                reciprocal(i)
-            if i >= 4:
-                add_bias_and_store(i - 4, 0)
-            if i < TILES:
-                normalise(i)
-            if i == 1:
-                keep_bias()
-            if i >= 4:
-                add_bias_and_store(i - 4, 1)
-            if i + 2 < TILES:
-                if (i + 2) % ROWS == 0:
-                    transpose_vk((i + 2) // ROWS)
-                transpose_q(i + 2)
-            if 1 <= i < TILES + 1:
-                transpose_a(i - 1)
+        nq = [0]
+
+        def tq(i, tag=None):
+            if i % ROWS == 0 and i > 0:
+                transpose_vk(i // ROWS)
+            transpose_q(i, tag)
+            copy_q(i, tag is not None)
+            if i == 0:
+                transpose_vk(0)
+                transpose_k_sum()
+
+        def n2(i):
+            if FILL_V5 and (i < FILL_V5 or i >= TILES - 1):
+                norm_vector(i, 2)
+            else:
+                norm_scalar(i, 2)
+
+        STAGE = {
+            "R": read_out, "den": den_add, "rec": reciprocal, "na": new_a,
+            "nA0": lambda i: norm_scalar(i, 0), "n2": n2, "nV1": lambda i: norm_vector(i, 1),
+            "TA": transpose_a, "cA": copy_a, "TQ": tq, "cQ": copy_q, "qz": quantise,
+            "P": project, "P0": lambda i: project(i, (0,)), "P1": lambda i: project(i, (1,)),
+            "b0": lambda i: add_bias_and_store(i, 0), "b1": lambda i: add_bias_and_store(i, 1),
+        }
+        warm_up(WARM0)
+        for j in range(PRO):
+            tq(j)
+            warm_up(WARM1)
+        nq[0] = PRO
+        maxlag = max(l for (n, l) in TEMPLATE)
+        for i in range(TILES + maxlag):
+            for (n, lag) in TEMPLATE:
+                if n == "Q":
+                    if nq[0] < TILES:
+                        tq(nq[0])
+                        nq[0] += 1
+                elif n == "X":
+                    if i < len(XTRA) and XTRA[i] and nq[0] < TILES:
+                        tq(nq[0], XTRA[i])
+                        nq[0] += 1
+                elif n == "bias":
+                    if i == lag:
+                        spread_bias()
+                elif n == "kbias":
+                    if i == lag:
+                        keep_bias()
+                elif n == "W":
+                    if i < len(WARM_FILL):
+                        warm_up(WARM_FILL[i][lag])
+                elif 0 <= i - lag < TILES:
+                    STAGE[n](i - lag)

@@ -42,12 +42,14 @@ ORDER = 0
 DRAIN_BANKS = 1
 PRO = 2
 WARM1 = 0
-TEMPLATE = (("R", 0), ("den", 0), ("bias", 1), ("P", 4), ("qz", 3), ("rec", 0), ("b0", 4), ("na", 0), ("nA0", 0), ("n2", 0), ("nV1", 0), ("kbias", 1), ("b1", 4), ("Q", 0), ("TA", 1), ("cA", 1))
-LOADS = "q00 v0 ks bias q01 q02 q03 v1 h10 h11 ws ww v2 h20 h21 v3 h30 h31"
+TEMPLATE = (("R", 0), ("den", 0), ("bias", 1), ("P", 3), ("qz", 2), ("rec", 0), ("b0", 3), ("na", 0), ("nA0", 0), ("n2", 0), ("nV1", 0), ("kbias", 1), ("b1", 3), ("TA", 1), ("cA", 1), ("Q", 0))
+LOADS = "q00 v0 ks q01 q02 q03 v1 h10 h11 ws ww bbc v2 h20 h21 v3 h30 h31"
 HEAD_BANKS = 1
 XTRA = ()
 QV_LO = 2
-QV_HI = 6
+QV_HI = 5
+BIAS_DMA = 1
+LAST_TA_SPLIT = 1
 
 
 def tile_lineartransformerblock_pc_kernel(tc, q_feat, vk, k_sum, Wo_words, Wo_scales, bo, out):
@@ -93,6 +95,8 @@ def tile_lineartransformerblock_pc_kernel(tc, q_feat, vk, k_sum, Wo_words, Wo_sc
             load_q(b, 0)
             load_q(b, 1)
 
+        bias_bc = keep.tile([P, C], BF16, name="bias_bc")
+
         def load_ws():
             for quad in range(4):
                 nc.sync.dma_start(
@@ -118,6 +122,8 @@ def tile_lineartransformerblock_pc_kernel(tc, q_feat, vk, k_sum, Wo_words, Wo_sc
                 nc.sync.dma_start(out=ks_sb[0 : B * H, :], in_=k_sum.rearrange("b h d -> (b h) d"))
             elif tok == "bias":
                 nc.sync.dma_start(out=bias_row[0:1, :], in_=bo.rearrange("(o c) -> o c", o=1))
+            elif tok == "bbc":
+                nc.sync.dma_start(out=bias_bc[:], in_=bo.partition_broadcast(P))
             elif tok == "ws":
                 load_ws()
             elif tok == "ww":
@@ -329,7 +335,7 @@ def tile_lineartransformerblock_pc_kernel(tc, q_feat, vk, k_sum, Wo_words, Wo_sc
             if nh == 0:
                 out_sb[i] = work.tile([P, C], F32, name="out_sb")
             cols = slice(nh * N_MX, (nh + 1) * N_MX)
-            nc.vector.tensor_tensor(out=out_sb[i][:, cols], in0=out_ps[i][nh][:], in1=bias_sb[:, cols], op=ALU.add)
+            nc.vector.tensor_tensor(out=out_sb[i][:, cols], in0=out_ps[i][nh][:], in1=(bias_bc if BIAS_DMA else bias_sb)[:, cols], op=ALU.add)
             b, r = divmod(i, ROWS)
             nc.sync.dma_start(out=out[b].rearrange("(p r) c -> r p c", r=ROWS)[r][:, cols], in_=out_sb[i][:, cols])
 
@@ -374,13 +380,20 @@ def tile_lineartransformerblock_pc_kernel(tc, q_feat, vk, k_sum, Wo_words, Wo_sc
                         tq(nq[0], XTRA[i])
                         nq[0] += 1
                 elif n == "bias":
-                    if i == lag:
+                    if i == lag and not BIAS_DMA:
                         spread_bias()
                 elif n == "kbias":
-                    if i == lag:
+                    if i == lag and not BIAS_DMA:
                         keep_bias()
                 elif n == "W":
                     if i < len(WARM_FILL):
                         warm_up(WARM_FILL[i][lag])
+                elif LAST_TA_SPLIT and i == TILES and n == "P":
+                    project(i - lag, (0,))
+                    transpose_a(TILES - 1)
+                    copy_a(TILES - 1)
+                    project(i - lag, (1,))
+                elif LAST_TA_SPLIT and i == TILES and n in ("TA", "cA"):
+                    pass
                 elif 0 <= i - lag < TILES:
                     STAGE[n](i - lag)

@@ -42,14 +42,22 @@ ORDER = 0
 DRAIN_BANKS = 1
 PRO = 2
 WARM1 = 0
-TEMPLATE = (("R", 0), ("den", 0), ("bias", 1), ("P", 3), ("qz", 2), ("rec", 0), ("b0", 3), ("na", 0), ("nA0", 0), ("n2", 0), ("nV1", 0), ("kbias", 1), ("b1", 3), ("TA", 1), ("cA", 1), ("Q", 0))
-LOADS = "q00 v0 ks q01 q02 q03 v1 h10 h11 ws ww bbc v2 h20 h21 v3 h30 h31"
+TEMPLATE = (("R", 0), ("den", 0), ("P", 3), ("qz", 2), ("rec", 0), ("b0", 3), ("na", 0), ("nA0", 0), ("n2", 0), ("nV1", 0), ("b1", 3), ("TA", 1), ("cA", 1), ("kb1", 1), ("Q", 0), ("bias", 0), ("kb0", 0))
+LOADS = "q00 v0 ks bias q01 q02 q03 v1 q10 ws ww q11 q12 q13 v2 h20 h21 v3 h30 h31"
 HEAD_BANKS = 1
 XTRA = ()
 QV_LO = 2
 QV_HI = 5
-BIAS_DMA = 1
+BIAS_DMA = 0
 LAST_TA_SPLIT = 1
+VK_EARLY = {}
+TEMPLATE_FILL = ()
+FILL_STEPS = 3
+DRAIN_FROM = 99
+WEAVE_END_MM = 1
+WQ_LEAD = 1
+WQ_GROUPS = (0, 1)
+KB_ACT = 1
 
 
 def tile_lineartransformerblock_pc_kernel(tc, q_feat, vk, k_sum, Wo_words, Wo_scales, bo, out):
@@ -154,9 +162,12 @@ def tile_lineartransformerblock_pc_kernel(tc, q_feat, vk, k_sum, Wo_words, Wo_sc
                 )
                 bias_ps.append(bank)
 
-        def keep_bias():
-            for nh in range(N_HALVES):
-                nc.vector.tensor_copy(out=bias_sb[:, nh * N_MX : (nh + 1) * N_MX], in_=bias_ps[nh][:])
+        def keep_bias(halves=(0, 1)):
+            for nh in halves:
+                if KB_ACT:
+                    nc.scalar.copy(out=bias_sb[:, nh * N_MX : (nh + 1) * N_MX], in_=bias_ps[nh][:])
+                else:
+                    nc.vector.tensor_copy(out=bias_sb[:, nh * N_MX : (nh + 1) * N_MX], in_=bias_ps[nh][:])
 
         warm = keep.tile([P, 1], F32, name="warm")
         nc.vector.memset(warm[:], 0.0)
@@ -175,6 +186,8 @@ def tile_lineartransformerblock_pc_kernel(tc, q_feat, vk, k_sum, Wo_words, Wo_sc
         def transpose_vk(b):
             if HEAD_BANKS and b == 0:
                 vk_ps = ps_one.tile([P, H, P], BF16, name="vk_ps", tag="a")
+            elif b in VK_EARLY:
+                vk_ps = ps_one.tile([P, H, P], BF16, name="vk_ps", tag="o%d" % (b % 2))
             else:
                 vk_ps = ps_t.tile([P, H, P], BF16, name="vk_ps", tag="t")
             for h in range(H):
@@ -212,10 +225,12 @@ def tile_lineartransformerblock_pc_kernel(tc, q_feat, vk, k_sum, Wo_words, Wo_sc
             else:
                 nc.scalar.copy(out=q_t[i][:], in_=q_ps[:])
 
-        def read_out(i):
+        def read_out(i, groups=(0, 1, 2)):
             b = i // ROWS
-            hs_ps[i] = []
-            for k, heads in enumerate(BANK_HEADS):
+            if 0 in groups:
+                hs_ps[i] = []
+            for k in groups:
+                heads = BANK_HEADS[k]
                 if HS_BUFS == 4:
                     bank = ps_one.tile([P, 3, D + 1], F32, name="hs_ps", tag="hs", bufs=4)
                 else:
@@ -230,18 +245,72 @@ def tile_lineartransformerblock_pc_kernel(tc, q_feat, vk, k_sum, Wo_words, Wo_sc
                     )
                 hs_ps[i].append(bank)
 
-        def den_add(i):
-            den = work.tile([P, H], F32, name="den")
-            for k, heads in enumerate(BANK_HEADS):
+        def mm_list(i, groups):
+            b = i // ROWS
+            if 0 in groups:
+                hs_ps[i] = []
+
+            def one(k, slot, h):
+                if slot == 0:
+                    bank = ps_one.tile([P, 3, D + 1], F32, name="hs_ps", tag="hs%d" % k)
+                    hs_ps[i].append(bank)
+                nc.tensor.matmul(
+                    out=hs_ps[i][k][:, slot, :], lhsT=q_t[i][:, h, :], rhs=vk_t[:, b * H + h, 0 : D + 1], start=True, stop=True
+                )
+
+            return [(one, (k, slot, h)) for k in groups for slot, h in enumerate(BANK_HEADS[k])]
+
+        def tq_list(i):
+            b, r = divmod(i, ROWS)
+
+            def one(h):
+                if h == 0:
+                    q_pss[i] = ps_t.tile([P, H, P], BF16, name="q_ps", tag="t")
+                nc.tensor.transpose(out=q_pss[i][:, h, :], in_=q_sb[b][:, h, r, :], identity=ident_bf[:])
+
+            return [(one, (h,)) for h in range(H)]
+
+        def ta_list(i):
+            def one(g, u):
+                if g == 0 and u == 0:
+                    a_pss[i] = ps_one.tile([P, PASSES, 2, P], F32, name="a_ps", tag="a")
+                nc.tensor.transpose(
+                    out=a_pss[i][:, g, u, :],
+                    in_=a_sb[i][:, g, u, :, :].rearrange("p h w -> p (h w)").bitcast(F32),
+                    identity=ident_f32[:],
+                )
+
+            return [(one, (g, u)) for g in range(PASSES) for u in range(2)]
+
+        def weave(first, second, lead):
+            seq = list(first[:lead])
+            rest = list(first[lead:])
+            other = list(second)
+            while rest or other:
+                if other:
+                    seq.append(other.pop(0))
+                if rest:
+                    seq.append(rest.pop(0))
+            for fn, args in seq:
+                fn(*args)
+
+        def den_add(i, groups=(0, 1, 2)):
+            if 0 in groups:
+                den_sb[i] = work.tile([P, H], F32, name="den")
+            den = den_sb[i]
+            for k in groups:
+                heads = BANK_HEADS[k]
                 nc.vector.tensor_scalar_add(
                     out=den[:, 3 * k : 3 * k + len(heads)], in0=hs_ps[i][k][:, 0 : len(heads), D], scalar1=EPS
                 )
             den_sb[i] = den
 
-        def reciprocal(i):
-            r_den[i] = work.tile([P, H], F32, name="r_den")
+        def reciprocal(i, groups=(0, 1, 2)):
+            if 0 in groups:
+                r_den[i] = work.tile([P, H], F32, name="r_den")
             if SPLIT_RECIP:
-                for k, heads in enumerate(BANK_HEADS):
+                for k in groups:
+                    heads = BANK_HEADS[k]
                     cols = slice(3 * k, 3 * k + len(heads))
                     nc.vector.reciprocal(out=r_den[i][:, cols], in_=den_sb[i][:, cols])
             else:
@@ -342,7 +411,7 @@ def tile_lineartransformerblock_pc_kernel(tc, q_feat, vk, k_sum, Wo_words, Wo_sc
         nq = [0]
 
         def tq(i, tag=None):
-            if i % ROWS == 0 and i > 0:
+            if i % ROWS == 0 and i > 0 and (i // ROWS) not in VK_EARLY:
                 transpose_vk(i // ROWS)
             transpose_q(i, tag)
             copy_q(i, tag is not None)
@@ -358,6 +427,9 @@ def tile_lineartransformerblock_pc_kernel(tc, q_feat, vk, k_sum, Wo_words, Wo_sc
 
         STAGE = {
             "R": read_out, "den": den_add, "rec": reciprocal, "na": new_a,
+            "Ra": lambda i: read_out(i, (0, 1)), "Rb": lambda i: read_out(i, (2,)),
+            "den01": lambda i: den_add(i, (0, 1)), "den2": lambda i: den_add(i, (2,)),
+            "rec01": lambda i: reciprocal(i, (0, 1)), "rec2": lambda i: reciprocal(i, (2,)),
             "nA0": lambda i: norm_scalar(i, 0), "n2": n2, "nV1": lambda i: norm_vector(i, 1),
             "TA": transpose_a, "cA": copy_a, "TQ": tq, "cQ": copy_q, "qz": quantise,
             "P": project, "P0": lambda i: project(i, (0,)), "P1": lambda i: project(i, (1,)),
@@ -370,7 +442,7 @@ def tile_lineartransformerblock_pc_kernel(tc, q_feat, vk, k_sum, Wo_words, Wo_sc
         nq[0] = PRO
         maxlag = max(l for (n, l) in TEMPLATE)
         for i in range(TILES + maxlag):
-            for (n, lag) in TEMPLATE:
+            for (n, lag) in (TEMPLATE_FILL if (TEMPLATE_FILL and (i < FILL_STEPS or i >= DRAIN_FROM)) else TEMPLATE):
                 if n == "Q":
                     if nq[0] < TILES:
                         tq(nq[0])
@@ -379,12 +451,42 @@ def tile_lineartransformerblock_pc_kernel(tc, q_feat, vk, k_sum, Wo_words, Wo_sc
                     if i < len(XTRA) and XTRA[i] and nq[0] < TILES:
                         tq(nq[0], XTRA[i])
                         nq[0] += 1
+                elif n == "WQ":
+                    j = i + WQ_LEAD
+                    ts = []
+                    if j < TILES:
+                        if j % ROWS == 0:
+                            transpose_vk(j // ROWS)
+                        ts = tq_list(j)
+                    ms = mm_list(i, WQ_GROUPS) if i < TILES else []
+                    if WEAVE_END_MM:
+                        weave(ts, ms, max(0, len(ts) - len(ms) + 1) if ms else len(ts))
+                    else:
+                        weave(ts, ms, lag)
+                    nq[0] = max(nq[0], j + 1)
+                elif n == "cQ1":
+                    if i + WQ_LEAD < TILES:
+                        copy_q(i + WQ_LEAD)
+                elif n == "WA":
+                    ms = mm_list(i, (2,)) if i < TILES else []
+                    ts = ta_list(i - 1) if 0 <= i - 1 < TILES else []
+                    weave(ms, ts, 1 if ms else 0)
+                elif n == "VK":
+                    for bb in VK_EARLY:
+                        if VK_EARLY[bb] == i:
+                            transpose_vk(bb)
                 elif n == "bias":
                     if i == lag and not BIAS_DMA:
                         spread_bias()
                 elif n == "kbias":
                     if i == lag and not BIAS_DMA:
                         keep_bias()
+                elif n == "kb0":
+                    if i == lag and not BIAS_DMA:
+                        keep_bias((0,))
+                elif n == "kb1":
+                    if i == lag and not BIAS_DMA:
+                        keep_bias((1,))
                 elif n == "W":
                     if i < len(WARM_FILL):
                         warm_up(WARM_FILL[i][lag])

@@ -58,6 +58,7 @@ WEAVE_END_MM = 1
 WQ_LEAD = 1
 WQ_GROUPS = (0, 1)
 KB_ACT = 1
+HS_PITCH = D + 2
 
 
 def tile_lineartransformerblock_pc_kernel(tc, q_feat, vk, k_sum, Wo_words, Wo_scales, bo, out):
@@ -232,12 +233,12 @@ def tile_lineartransformerblock_pc_kernel(tc, q_feat, vk, k_sum, Wo_words, Wo_sc
             for k in groups:
                 heads = BANK_HEADS[k]
                 if HS_BUFS == 4:
-                    bank = ps_one.tile([P, 3, D + 1], F32, name="hs_ps", tag="hs", bufs=4)
+                    bank = ps_one.tile([P, 3, HS_PITCH], F32, name="hs_ps", tag="hs", bufs=4)
                 else:
-                    bank = ps_one.tile([P, 3, D + 1], F32, name="hs_ps", tag="hs%d" % k)
+                    bank = ps_one.tile([P, 3, HS_PITCH], F32, name="hs_ps", tag="hs%d" % k)
                 for slot, h in enumerate(heads):
                     nc.tensor.matmul(
-                        out=bank[:, slot, :],
+                        out=bank[:, slot, 0 : D + 1],
                         lhsT=q_t[i][:, h, :],
                         rhs=vk_t[:, b * H + h, 0 : D + 1],
                         start=True,
@@ -252,10 +253,10 @@ def tile_lineartransformerblock_pc_kernel(tc, q_feat, vk, k_sum, Wo_words, Wo_sc
 
             def one(k, slot, h):
                 if slot == 0:
-                    bank = ps_one.tile([P, 3, D + 1], F32, name="hs_ps", tag="hs%d" % k)
+                    bank = ps_one.tile([P, 3, HS_PITCH], F32, name="hs_ps", tag="hs%d" % k)
                     hs_ps[i].append(bank)
                 nc.tensor.matmul(
-                    out=hs_ps[i][k][:, slot, :], lhsT=q_t[i][:, h, :], rhs=vk_t[:, b * H + h, 0 : D + 1], start=True, stop=True
+                    out=hs_ps[i][k][:, slot, 0 : D + 1], lhsT=q_t[i][:, h, :], rhs=vk_t[:, b * H + h, 0 : D + 1], start=True, stop=True
                 )
 
             return [(one, (k, slot, h)) for k in groups for slot, h in enumerate(BANK_HEADS[k])]

@@ -42,7 +42,7 @@ ORDER = 0
 DRAIN_BANKS = 1
 PRO = 2
 WARM1 = 0
-TEMPLATE = (("R", 0), ("den", 0), ("P", 3), ("qz", 2), ("rec", 0), ("b0", 3), ("na", 0), ("nA0", 0), ("n2", 0), ("nV1", 0), ("b1", 3), ("TA", 1), ("cA", 1), ("kb1", 1), ("Q", 0), ("bias", 0), ("kb0", 0))
+TEMPLATE = (("Ra", 0), ("den01", 0), ("P", 3), ("Rb", 0), ("qz", 2), ("rec01", 0), ("na", 0), ("nA0", 0), ("b0", 3), ("nV1", 0), ("den2", 0), ("b1", 3), ("rec2", 0), ("TA", 1), ("cA", 1), ("n2", 0), ("Q", 0))
 LOADS = "q00 v0 ks bias q01 q02 q03 v1 q10 ws ww q11 q12 q13 v2 h20 h21 v3 h30 h31"
 HEAD_BANKS = 1
 XTRA = ()
@@ -51,7 +51,7 @@ QV_HI = 5
 BIAS_DMA = 0
 LAST_TA_SPLIT = 1
 VK_EARLY = {}
-TEMPLATE_FILL = ()
+TEMPLATE_FILL = (("R", 0), ("den", 0), ("P", 3), ("qz", 2), ("rec", 0), ("b0", 3), ("na", 0), ("nA0", 0), ("n2", 0), ("nV1", 0), ("b1", 3), ("TA", 1), ("cA", 1), ("kb1", 1), ("Q", 0), ("bias", 0), ("kb0", 0))
 FILL_STEPS = 3
 DRAIN_FROM = 99
 WEAVE_END_MM = 1
@@ -59,6 +59,9 @@ WQ_LEAD = 1
 WQ_GROUPS = (0, 1)
 KB_ACT = 1
 HS_PITCH = D + 2
+TAIL_SPLIT = 1
+TAIL_FROM = 1
+HEAD_SPLIT = 0
 
 
 def tile_lineartransformerblock_pc_kernel(tc, q_feat, vk, k_sum, Wo_words, Wo_scales, bo, out):
@@ -121,7 +124,13 @@ def tile_lineartransformerblock_pc_kernel(tc, q_feat, vk, k_sum, Wo_words, Wo_sc
                 )
 
         for tok in LOADS.split():
-            if tok[0] == "q":
+            if tok in ("qa", "qb"):
+                hh = slice(0, 4) if tok == "qa" else slice(4, 8)
+                nc.sync.dma_start(out=q_sb[0][:, hh, 0, :], in_=q_feat[0, hh].rearrange("h (p r) d -> r p h d", r=ROWS)[0])
+            elif tok in ("va", "vb"):
+                hh = slice(0, 4) if tok == "va" else slice(4, 8)
+                nc.sync.dma_start(out=vk_sb[0][:, hh, :], in_=vk[0, hh].rearrange("h n d -> n h d"))
+            elif tok[0] == "q":
                 load_q_tile(int(tok[1]), int(tok[2]))
             elif tok[0] == "v":
                 load_vk(int(tok[1]))
@@ -404,10 +413,13 @@ def tile_lineartransformerblock_pc_kernel(tc, q_feat, vk, k_sum, Wo_words, Wo_sc
         def add_bias_and_store(i, nh):
             if nh == 0:
                 out_sb[i] = work.tile([P, C], F32, name="out_sb")
-            cols = slice(nh * N_MX, (nh + 1) * N_MX)
-            nc.vector.tensor_tensor(out=out_sb[i][:, cols], in0=out_ps[i][nh][:], in1=(bias_bc if BIAS_DMA else bias_sb)[:, cols], op=ALU.add)
             b, r = divmod(i, ROWS)
-            nc.sync.dma_start(out=out[b].rearrange("(p r) c -> r p c", r=ROWS)[r][:, cols], in_=out_sb[i][:, cols])
+            pieces = TAIL_SPLIT if (i == TILES - 1 and nh >= TAIL_FROM) else 1
+            w = N_MX // pieces
+            for q in range(pieces):
+                cols = slice(nh * N_MX + q * w, nh * N_MX + (q + 1) * w)
+                nc.vector.tensor_tensor(out=out_sb[i][:, cols], in0=out_ps[i][nh][:, q * w : (q + 1) * w], in1=(bias_bc if BIAS_DMA else bias_sb)[:, cols], op=ALU.add)
+                nc.sync.dma_start(out=out[b].rearrange("(p r) c -> r p c", r=ROWS)[r][:, cols], in_=out_sb[i][:, cols])
 
         nq = [0]
 
@@ -436,8 +448,24 @@ def tile_lineartransformerblock_pc_kernel(tc, q_feat, vk, k_sum, Wo_words, Wo_sc
             "P": project, "P0": lambda i: project(i, (0,)), "P1": lambda i: project(i, (1,)),
             "b0": lambda i: add_bias_and_store(i, 0), "b1": lambda i: add_bias_and_store(i, 1),
         }
+        def head():
+            q_t[0] = work.tile([P, H, P], BF16, name="q_t", bufs=TILES)
+            for half, vtag in ((0, "a"), (1, "o1")):
+                q_ps = ps_t.tile([P, 4, P], BF16, name="q_ps", tag="t")
+                for h in range(4):
+                    nc.tensor.transpose(out=q_ps[:, h, :], in_=q_sb[0][:, 4 * half + h, 0, :], identity=ident_bf[:])
+                nc.scalar.copy(out=q_t[0][:, 4 * half : 4 * half + 4, :], in_=q_ps[:])
+                vk_ps = ps_one.tile([P, 4, P], BF16, name="vk_ps", tag=vtag)
+                for h in range(4):
+                    nc.tensor.transpose(out=vk_ps[:, h, :], in_=vk_sb[0][:, 4 * half + h, :], identity=order_n[:])
+                nc.vector.tensor_copy(out=vk_t[:, 4 * half : 4 * half + 4, 0:D], in_=vk_ps[:])
+                if half == 0:
+                    transpose_k_sum()
+
         warm_up(WARM0)
-        for j in range(PRO):
+        if HEAD_SPLIT:
+            head()
+        for j in range(1 if HEAD_SPLIT else 0, PRO):
             tq(j)
             warm_up(WARM1)
         nq[0] = PRO

@@ -31,7 +31,7 @@ FLOPS = 2 * B * S * (H * D) * C + 2 * B * H * S * D * D + 2 * B * H * S * D
 
 HS_BUFS = 3
 LP = 4
-WARM0 = 0
+WARM0 = 6
 WARM_FILL = ()
 SPLIT_RECIP = 1
 LEAD = (2, 2, 2, 2)
@@ -41,7 +41,7 @@ FILL_V5 = 0
 ORDER = 0
 DRAIN_BANKS = 1
 PRO = 2
-WARM1 = 0
+WARM1 = (0, 0, 0)
 TEMPLATE = (("Ra", 0), ("den01", 0), ("P", 3), ("Rb", 0), ("qz", 2), ("rec01", 0), ("na", 0), ("nA0", 0), ("b0", 3), ("nV1", 0), ("den2", 0), ("b1", 3), ("rec2", 0), ("TA", 1), ("cA", 1), ("n2", 0), ("Q", 0))
 LOADS = "q00 v0 ks bias q01 q02 q03 v1 q10 ws ww q11 q12 q13 v2 h20 h21 v3 h30 h31"
 HEAD_BANKS = 1
@@ -49,9 +49,9 @@ XTRA = ()
 QV_LO = 2
 QV_HI = 5
 BIAS_DMA = 0
-LAST_TA_SPLIT = 1
+LAST_TA_SPLIT = 0
 VK_EARLY = {}
-TEMPLATE_FILL = (("R", 0), ("den", 0), ("P", 3), ("qz", 2), ("rec", 0), ("b0", 3), ("na", 0), ("nA0", 0), ("n2", 0), ("nV1", 0), ("b1", 3), ("TA", 1), ("cA", 1), ("kb1", 1), ("Q", 0), ("bias", 0), ("kb0", 0))
+TEMPLATE_FILL = (("R", 0), ("den", 0), ("rec", 0), ("na", 0), ("nA0", 0), ("n2", 0), ("nV1", 0), ("P", 3), ("qz", 2), ("b0", 3), ("b1", 3), ("TA", 1), ("cA", 1), ("kb1", 1), ("Q", 0), ("bias", 0), ("kb0", 0))
 FILL_STEPS = 3
 DRAIN_FROM = 99
 WEAVE_END_MM = 1
@@ -62,6 +62,11 @@ HS_PITCH = D + 2
 TAIL_SPLIT = 1
 TAIL_FROM = 1
 HEAD_SPLIT = 0
+SLOW_FROM = 99
+SLOW_TO = 99
+EXTRA_STEPS = 0
+RING_FROM = 999
+TEMPLATE_DRAIN = ()
 
 
 def tile_lineartransformerblock_pc_kernel(tc, q_feat, vk, k_sum, Wo_words, Wo_scales, bo, out):
@@ -147,9 +152,9 @@ def tile_lineartransformerblock_pc_kernel(tc, q_feat, vk, k_sum, Wo_words, Wo_sc
             elif tok == "ww":
                 load_ww()
 
-        def warm_up(n):
+        def warm_up(n, tag=None):
             for k in range(n):
-                junk = ps_one.tile([P, N_MX], F32, name="junk", tag="o%d" % (k % 2))
+                junk = ps_one.tile([P, N_MX], F32, name="junk", tag=tag or "o%d" % (k % 2))
                 nc.tensor.matmul(out=junk[:], lhsT=zeros[:, 0:P], rhs=zeros[:], start=True, stop=True)
 
         ident_bf = keep.tile([P, P], BF16, name="ident_bf")
@@ -393,7 +398,9 @@ def tile_lineartransformerblock_pc_kernel(tc, q_feat, vk, k_sum, Wo_words, Wo_sc
             if 0 in halves:
                 out_ps[i] = []
             for nh in halves:
-                if DRAIN_BANKS and i == TILES - 2:
+                if RING_FROM <= 2 * i + nh:
+                    acc = ps_one.tile([P, N_MX], F32, name="acc", tag=("o0", "o1", "hs0", "hs1", "hs2")[(2 * i + nh - RING_FROM) % 5])
+                elif DRAIN_BANKS and i == TILES - 2:
                     acc = ps_one.tile([P, N_MX], F32, name="acc", tag="hs%d" % nh)
                 else:
                     acc = ps_one.tile([P, N_MX], F32, name="acc", tag="o%d" % nh)
@@ -467,11 +474,13 @@ def tile_lineartransformerblock_pc_kernel(tc, q_feat, vk, k_sum, Wo_words, Wo_sc
             head()
         for j in range(1 if HEAD_SPLIT else 0, PRO):
             tq(j)
-            warm_up(WARM1)
+            warm_up(WARM1[j], "o1")
         nq[0] = PRO
         maxlag = max(l for (n, l) in TEMPLATE)
-        for i in range(TILES + maxlag):
-            for (n, lag) in (TEMPLATE_FILL if (TEMPLATE_FILL and (i < FILL_STEPS or i >= DRAIN_FROM)) else TEMPLATE):
+        ph = [0]
+        bh = [0]
+        for i in range(TILES + maxlag + EXTRA_STEPS):
+            for (n, lag) in (TEMPLATE_DRAIN if (TEMPLATE_DRAIN and i >= DRAIN_FROM) else TEMPLATE_FILL if (TEMPLATE_FILL and (i < FILL_STEPS or i >= DRAIN_FROM)) else TEMPLATE):
                 if n == "Q":
                     if nq[0] < TILES:
                         tq(nq[0])
@@ -498,8 +507,18 @@ def tile_lineartransformerblock_pc_kernel(tc, q_feat, vk, k_sum, Wo_words, Wo_sc
                         copy_q(i + WQ_LEAD)
                 elif n == "WA":
                     ms = mm_list(i, (2,)) if i < TILES else []
-                    ts = ta_list(i - 1) if 0 <= i - 1 < TILES else []
+                    ts = ta_list(i - 1) if (0 <= i - 1 < TILES and not (LAST_TA_SPLIT and i == TILES)) else []
                     weave(ms, ts, 1 if ms else 0)
+                elif n == "PH":
+                    count = 2 if (i < SLOW_FROM or i >= SLOW_TO) else 1
+                    for k in range(count):
+                        if ph[0] < 2 * TILES and ph[0] // 2 <= i - lag:
+                            project(ph[0] // 2, (ph[0] % 2,))
+                            ph[0] += 1
+                elif n == "BH":
+                    if bh[0] < ph[0]:
+                        add_bias_and_store(bh[0] // 2, bh[0] % 2)
+                        bh[0] += 1
                 elif n == "VK":
                     for bb in VK_EARLY:
                         if VK_EARLY[bb] == i:
@@ -518,7 +537,7 @@ def tile_lineartransformerblock_pc_kernel(tc, q_feat, vk, k_sum, Wo_words, Wo_sc
                         keep_bias((1,))
                 elif n == "W":
                     if i < len(WARM_FILL):
-                        warm_up(WARM_FILL[i][lag])
+                        warm_up(WARM_FILL[i][lag], "o0")
                 elif LAST_TA_SPLIT and i == TILES and n == "P":
                     project(i - lag, (0,))
                     transpose_a(TILES - 1)

@@ -67,6 +67,12 @@ SLOW_TO = 99
 EXTRA_STEPS = 0
 RING_FROM = 999
 TEMPLATE_DRAIN = ()
+P_GOUTER = 0
+WARM_HEAD = (0, 0, 0)
+ALT_TAGS = {1: ("o0", "o1", "t")}
+SEQ = "TQ:0 B:0o0 B:1o1 kbA:0 kbA:1 TQ:1 R:0 den:0 rec:0 na:0 nA0:0 n2:0 nV1:0 TQ:2 R:1 den:1 rec:1 na:1 nA0:1 TA:0 cA:0 n2:1 nV1:1 TQ:3 R:2 den:2 rec:2 na:2 nA0:2 n2:2 nV1:2 qz:0 TA:1 cA:1 TQ:4"
+FIRST_STEP = 3
+KS_TAG = "hs2"
 
 
 def tile_lineartransformerblock_pc_kernel(tc, q_feat, vk, k_sum, Wo_words, Wo_scales, bo, out):
@@ -92,8 +98,10 @@ def tile_lineartransformerblock_pc_kernel(tc, q_feat, vk, k_sum, Wo_words, Wo_sc
         nc.vector.memset(ks_sb[:], 0.0)
         nc.vector.memset(w_scales[:].rearrange("p g n -> p (g n)").bitcast(I32), 0)
 
+        qsel = [nc.sync]
+
         def load_q_tile(b, r):
-            nc.sync.dma_start(
+            qsel[0].dma_start(
                 out=q_sb[b][:, :, r, :], in_=q_feat[b].rearrange("h (p r) d -> r p h d", r=ROWS)[r]
             )
 
@@ -105,7 +113,7 @@ def tile_lineartransformerblock_pc_kernel(tc, q_feat, vk, k_sum, Wo_words, Wo_sc
             )
 
         def load_vk(b):
-            nc.sync.dma_start(out=vk_sb[b][:], in_=vk[b].rearrange("h n d -> n h d"))
+            qsel[0].dma_start(out=vk_sb[b][:], in_=vk[b].rearrange("h n d -> n h d"))
 
         def load_batch(b):
             load_vk(b)
@@ -129,6 +137,10 @@ def tile_lineartransformerblock_pc_kernel(tc, q_feat, vk, k_sum, Wo_words, Wo_sc
                 )
 
         for tok in LOADS.split():
+            qsel[0] = nc.sync
+            if tok[-2:] == "@a":
+                qsel[0] = nc.scalar
+                tok = tok[:-2]
             if tok in ("qa", "qb"):
                 hh = slice(0, 4) if tok == "qa" else slice(4, 8)
                 nc.sync.dma_start(out=q_sb[0][:, hh, 0, :], in_=q_feat[0, hh].rearrange("h (p r) d -> r p h d", r=ROWS)[0])
@@ -142,9 +154,9 @@ def tile_lineartransformerblock_pc_kernel(tc, q_feat, vk, k_sum, Wo_words, Wo_sc
             elif tok[0] == "h":
                 load_q(int(tok[1]), int(tok[2]))
             elif tok == "ks":
-                nc.sync.dma_start(out=ks_sb[0 : B * H, :], in_=k_sum.rearrange("b h d -> (b h) d"))
+                qsel[0].dma_start(out=ks_sb[0 : B * H, :], in_=k_sum.rearrange("b h d -> (b h) d"))
             elif tok == "bias":
-                nc.sync.dma_start(out=bias_row[0:1, :], in_=bo.rearrange("(o c) -> o c", o=1))
+                qsel[0].dma_start(out=bias_row[0:1, :], in_=bo.rearrange("(o c) -> o c", o=1))
             elif tok == "bbc":
                 nc.sync.dma_start(out=bias_bc[:], in_=bo.partition_broadcast(P))
             elif tok == "ws":
@@ -177,6 +189,20 @@ def tile_lineartransformerblock_pc_kernel(tc, q_feat, vk, k_sum, Wo_words, Wo_sc
                 )
                 bias_ps.append(bank)
 
+        def spread_half(nh, tag):
+            while len(bias_ps) < 2:
+                bias_ps.append(None)
+            bias_ps[nh] = ps_one.tile([P, N_MX], F32, name="bias_ps", tag=tag)
+            nc.tensor.matmul(
+                out=bias_ps[nh][:], lhsT=ones_bf[:], rhs=bias_row[:, nh * N_MX : (nh + 1) * N_MX], start=True, stop=True
+            )
+
+        def keep_half(nh, on_vector):
+            if on_vector:
+                nc.vector.tensor_copy(out=bias_sb[:, nh * N_MX : (nh + 1) * N_MX], in_=bias_ps[nh][:])
+            else:
+                nc.scalar.copy(out=bias_sb[:, nh * N_MX : (nh + 1) * N_MX], in_=bias_ps[nh][:])
+
         def keep_bias(halves=(0, 1)):
             for nh in halves:
                 if KB_ACT:
@@ -192,7 +218,7 @@ def tile_lineartransformerblock_pc_kernel(tc, q_feat, vk, k_sum, Wo_words, Wo_sc
 
         def transpose_k_sum():
             if HEAD_BANKS:
-                ks_ps = ps_one.tile([P, H, P], BF16, name="ks_ps", tag="o0")
+                ks_ps = ps_one.tile([P, H, P], BF16, name="ks_ps", tag=KS_TAG)
             else:
                 ks_ps = ps_t.tile([P, H, P], BF16, name="ks_ps", tag="t")
             nc.tensor.transpose(out=ks_ps[:, 0, :], in_=ks_sb[:], identity=ident_bf[:])
@@ -246,7 +272,10 @@ def tile_lineartransformerblock_pc_kernel(tc, q_feat, vk, k_sum, Wo_words, Wo_sc
                 hs_ps[i] = []
             for k in groups:
                 heads = BANK_HEADS[k]
-                if HS_BUFS == 4:
+                if i in ALT_TAGS:
+                    at = ALT_TAGS[i][k]
+                    bank = (ps_t if at == "t" else ps_one).tile([P, 3, HS_PITCH], F32, name="hs_ps", tag=at)
+                elif HS_BUFS == 4:
                     bank = ps_one.tile([P, 3, HS_PITCH], F32, name="hs_ps", tag="hs", bufs=4)
                 else:
                     bank = ps_one.tile([P, 3, HS_PITCH], F32, name="hs_ps", tag="hs%d" % k)
@@ -374,10 +403,10 @@ def tile_lineartransformerblock_pc_kernel(tc, q_feat, vk, k_sum, Wo_words, Wo_sc
                     )
             a_pss[i] = a_ps
 
-        def copy_a(i):
+        def copy_a(i, on_vector=False):
             a_ps = a_pss[i]
             grouped[i] = work.tile([P, PASSES, P, PACK], BF16, name="grouped", align_bytes=64)
-            nc.scalar.copy(
+            (nc.vector.tensor_copy if on_vector else nc.scalar.copy)(
                 out=grouped[i][:]
                 .rearrange("p g s t -> p (g s t)")
                 .bitcast(F32)
@@ -395,6 +424,21 @@ def tile_lineartransformerblock_pc_kernel(tc, q_feat, vk, k_sum, Wo_words, Wo_sc
             )
 
         def project(i, halves=(0, 1)):
+            if P_GOUTER and len(halves) == 2:
+                out_ps[i] = [ps_one.tile([P, N_MX], F32, name="acc", tag=("hs%d" if (DRAIN_BANKS and i == TILES - 2) else "o%d") % nh) for nh in halves]
+                for g in range(PASSES):
+                    tokens = slice(g * P, (g + 1) * P)
+                    for nh in halves:
+                        nc.tensor.matmul_mx(
+                            out=out_ps[i][nh][:],
+                            lhsT=codes[i][:, tokens].bitcast(FP8X4),
+                            lhsT_scale=a_scales[i][:, tokens],
+                            rhs=w_words[:, g, nh * N_MX * PACK : (nh + 1) * N_MX * PACK].bitcast(FP8X4),
+                            rhs_scale=w_scales[:, g, nh * N_MX : (nh + 1) * N_MX],
+                            start=(g == 0),
+                            stop=(g == PASSES - 1),
+                        )
+                return
             if 0 in halves:
                 out_ps[i] = []
             for nh in halves:
@@ -436,8 +480,12 @@ def tile_lineartransformerblock_pc_kernel(tc, q_feat, vk, k_sum, Wo_words, Wo_sc
             transpose_q(i, tag)
             copy_q(i, tag is not None)
             if i == 0:
+                warm_up(WARM_HEAD[0], "o1")
                 transpose_vk(0)
                 transpose_k_sum()
+                warm_up(WARM_HEAD[1], "o1")
+            if i == 1:
+                warm_up(WARM_HEAD[2], "o1")
 
         def n2(i):
             if FILL_V5 and (i < FILL_V5 or i >= TILES - 1):
@@ -451,7 +499,7 @@ def tile_lineartransformerblock_pc_kernel(tc, q_feat, vk, k_sum, Wo_words, Wo_sc
             "den01": lambda i: den_add(i, (0, 1)), "den2": lambda i: den_add(i, (2,)),
             "rec01": lambda i: reciprocal(i, (0, 1)), "rec2": lambda i: reciprocal(i, (2,)),
             "nA0": lambda i: norm_scalar(i, 0), "n2": n2, "nV1": lambda i: norm_vector(i, 1),
-            "TA": transpose_a, "cA": copy_a, "TQ": tq, "cQ": copy_q, "qz": quantise,
+            "TA": transpose_a, "cA": copy_a, "cAV": lambda i: copy_a(i, True), "TQ": tq, "cQ": copy_q, "qz": quantise,
             "P": project, "P0": lambda i: project(i, (0,)), "P1": lambda i: project(i, (1,)),
             "b0": lambda i: add_bias_and_store(i, 0), "b1": lambda i: add_bias_and_store(i, 1),
         }
@@ -470,16 +518,33 @@ def tile_lineartransformerblock_pc_kernel(tc, q_feat, vk, k_sum, Wo_words, Wo_sc
                     transpose_k_sum()
 
         warm_up(WARM0)
+        if SEQ:
+            for tok in SEQ.split():
+                n, arg = tok.split(":")
+                if n == "B":
+                    spread_half(int(arg[0]), arg[1:])
+                elif n == "kbA":
+                    keep_half(int(arg), False)
+                elif n == "kbV":
+                    keep_half(int(arg), True)
+                elif n == "TQ":
+                    tq(int(arg))
+                    nq[0] = int(arg) + 1
+                elif n == "W":
+                    warm_up(1, arg)
+                else:
+                    STAGE[n](int(arg))
         if HEAD_SPLIT:
             head()
-        for j in range(1 if HEAD_SPLIT else 0, PRO):
+        for j in range(1 if HEAD_SPLIT else 0, 0 if SEQ else PRO):
             tq(j)
             warm_up(WARM1[j], "o1")
-        nq[0] = PRO
+        if not SEQ:
+            nq[0] = PRO
         maxlag = max(l for (n, l) in TEMPLATE)
         ph = [0]
         bh = [0]
-        for i in range(TILES + maxlag + EXTRA_STEPS):
+        for i in range(FIRST_STEP, TILES + maxlag + EXTRA_STEPS):
             for (n, lag) in (TEMPLATE_DRAIN if (TEMPLATE_DRAIN and i >= DRAIN_FROM) else TEMPLATE_FILL if (TEMPLATE_FILL and (i < FILL_STEPS or i >= DRAIN_FROM)) else TEMPLATE):
                 if n == "Q":
                     if nq[0] < TILES:

@@ -25,54 +25,18 @@ N_HALVES = C // N_MX
 ROWS = S // P
 TILES = B * ROWS
 VK_PITCH = 136
+
+HS_PITCH = D + 2
 BANK_HEADS = ((0, 1, 2), (4, 5, 6), (3, 7))
+ALL_BANKS = (0, 1, 2)
+
+LAG = 3
+Q_AHEAD = 2
+WARM_UP_MATMULS = 6
+KEEP_WARM_MATMULS = 2
+OTHER_BANKS = {1: ("o0", "o1", "t"), TILES - 1: ("t", "t", "hs2")}
 
 FLOPS = 2 * B * S * (H * D) * C + 2 * B * H * S * D * D + 2 * B * H * S * D
-
-HS_BUFS = 3
-LP = 4
-WARM0 = 6
-WARM_FILL = ()
-SPLIT_RECIP = 1
-LEAD = (2, 2, 2, 2)
-LEAD_STEADY = 2
-QCOPY_V = 0
-FILL_V5 = 0
-ORDER = 0
-DRAIN_BANKS = 1
-PRO = 2
-WARM1 = (0, 0, 0)
-TEMPLATE = (("Ra", 0), ("den01", 0), ("P", 3), ("Rb", 0), ("qz", 2), ("rec01", 0), ("na", 0), ("nA0", 0), ("b0", 3), ("nV1", 0), ("den2", 0), ("b1", 3), ("rec2", 0), ("TA", 1), ("cA", 1), ("n2", 0), ("Q", 0))
-LOADS = "q00 v0 ks bias q01 q02 q03 v1 q10 ws ww q11 q12 q13 v2 h20 h21 v3 h30 h31"
-HEAD_BANKS = 1
-XTRA = ()
-QV_LO = 2
-QV_HI = 5
-BIAS_DMA = 0
-LAST_TA_SPLIT = 0
-VK_EARLY = {}
-TEMPLATE_FILL = (("R", 0), ("den", 0), ("rec", 0), ("na", 0), ("nA0", 0), ("n2", 0), ("nV1", 0), ("P", 3), ("qz", 2), ("b0", 3), ("b1", 3), ("TA", 1), ("cA", 1), ("kb1", 1), ("Q", 0), ("bias", 0), ("kb0", 0))
-FILL_STEPS = 3
-DRAIN_FROM = 99
-WEAVE_END_MM = 1
-WQ_LEAD = 1
-WQ_GROUPS = (0, 1)
-KB_ACT = 1
-HS_PITCH = D + 2
-TAIL_SPLIT = 1
-TAIL_FROM = 1
-HEAD_SPLIT = 0
-SLOW_FROM = 99
-SLOW_TO = 99
-EXTRA_STEPS = 0
-RING_FROM = 999
-TEMPLATE_DRAIN = ()
-P_GOUTER = 0
-WARM_HEAD = (0, 0, 0)
-ALT_TAGS = {1: ("o0", "o1", "t")}
-SEQ = "TQ:0 B:0o0 B:1o1 kbA:0 kbA:1 TQ:1 R:0 den:0 rec:0 na:0 nA0:0 n2:0 nV1:0 TQ:2 R:1 den:1 rec:1 na:1 nA0:1 TA:0 cA:0 n2:1 nV1:1 TQ:3 R:2 den:2 rec:2 na:2 nA0:2 n2:2 nV1:2 qz:0 TA:1 cA:1 TQ:4"
-FIRST_STEP = 3
-KS_TAG = "hs2"
 
 
 def tile_lineartransformerblock_pc_kernel(tc, q_feat, vk, k_sum, Wo_words, Wo_scales, bo, out):
@@ -92,20 +56,19 @@ def tile_lineartransformerblock_pc_kernel(tc, q_feat, vk, k_sum, Wo_words, Wo_sc
         w_scales = keep.tile([P, PASSES, C], U8, name="w_scales", align_bytes=64)
         ones_bf = keep.tile([P, P], BF16, name="ones_bf")
         zeros = keep.tile([P, N_MX], BF16, name="zeros")
+
         nc.vector.memset(zeros[:], 0.0)
         nc.vector.memset(ones_bf[:], 1.0)
         nc.vector.memset(bias_row[:], 0.0)
         nc.vector.memset(ks_sb[:], 0.0)
         nc.vector.memset(w_scales[:].rearrange("p g n -> p (g n)").bitcast(I32), 0)
 
-        qsel = [nc.sync]
-
         def load_q_tile(b, r):
-            qsel[0].dma_start(
+            nc.sync.dma_start(
                 out=q_sb[b][:, :, r, :], in_=q_feat[b].rearrange("h (p r) d -> r p h d", r=ROWS)[r]
             )
 
-        def load_q(b, half):
+        def load_q_heads(b, half):
             heads = slice(half * HEADS_PER_PASS, (half + 1) * HEADS_PER_PASS)
             nc.sync.dma_start(
                 out=q_sb[b][:, heads, :, :].rearrange("p h r d -> p h (r d)"),
@@ -113,61 +76,35 @@ def tile_lineartransformerblock_pc_kernel(tc, q_feat, vk, k_sum, Wo_words, Wo_sc
             )
 
         def load_vk(b):
-            qsel[0].dma_start(out=vk_sb[b][:], in_=vk[b].rearrange("h n d -> n h d"))
+            nc.sync.dma_start(out=vk_sb[b][:], in_=vk[b].rearrange("h n d -> n h d"))
 
-        def load_batch(b):
-            load_vk(b)
-            load_q(b, 0)
-            load_q(b, 1)
-
-        bias_bc = keep.tile([P, C], BF16, name="bias_bc")
-
-        def load_ws():
+        def load_w():
             for quad in range(4):
                 nc.sync.dma_start(
                     out=w_scales[32 * quad : 32 * quad + 4, :, :].bitcast(I32),
                     in_=Wo_scales[:, 4 * quad : 4 * quad + 4, :].rearrange("g r n -> r g n").bitcast(I32),
                 )
-
-        def load_ww():
             for g in range(PASSES):
                 nc.sync.dma_start(
                     out=w_words[:, g, :].bitcast(I32),
                     in_=Wo_words[g].rearrange("p n t -> p (n t)").bitcast(I32),
                 )
 
-        for tok in LOADS.split():
-            qsel[0] = nc.sync
-            if tok[-2:] == "@a":
-                qsel[0] = nc.scalar
-                tok = tok[:-2]
-            if tok in ("qa", "qb"):
-                hh = slice(0, 4) if tok == "qa" else slice(4, 8)
-                nc.sync.dma_start(out=q_sb[0][:, hh, 0, :], in_=q_feat[0, hh].rearrange("h (p r) d -> r p h d", r=ROWS)[0])
-            elif tok in ("va", "vb"):
-                hh = slice(0, 4) if tok == "va" else slice(4, 8)
-                nc.sync.dma_start(out=vk_sb[0][:, hh, :], in_=vk[0, hh].rearrange("h n d -> n h d"))
-            elif tok[0] == "q":
-                load_q_tile(int(tok[1]), int(tok[2]))
-            elif tok[0] == "v":
-                load_vk(int(tok[1]))
-            elif tok[0] == "h":
-                load_q(int(tok[1]), int(tok[2]))
-            elif tok == "ks":
-                qsel[0].dma_start(out=ks_sb[0 : B * H, :], in_=k_sum.rearrange("b h d -> (b h) d"))
-            elif tok == "bias":
-                qsel[0].dma_start(out=bias_row[0:1, :], in_=bo.rearrange("(o c) -> o c", o=1))
-            elif tok == "bbc":
-                nc.sync.dma_start(out=bias_bc[:], in_=bo.partition_broadcast(P))
-            elif tok == "ws":
-                load_ws()
-            elif tok == "ww":
-                load_ww()
-
-        def warm_up(n, tag=None):
-            for k in range(n):
-                junk = ps_one.tile([P, N_MX], F32, name="junk", tag=tag or "o%d" % (k % 2))
-                nc.tensor.matmul(out=junk[:], lhsT=zeros[:, 0:P], rhs=zeros[:], start=True, stop=True)
+        load_q_tile(0, 0)
+        load_vk(0)
+        nc.sync.dma_start(out=ks_sb[0 : B * H, :], in_=k_sum.rearrange("b h d -> (b h) d"))
+        nc.sync.dma_start(out=bias_row[0:1, :], in_=bo.rearrange("(o c) -> o c", o=1))
+        for r in range(1, ROWS):
+            load_q_tile(0, r)
+        load_vk(1)
+        load_q_tile(1, 0)
+        load_w()
+        for r in range(1, ROWS):
+            load_q_tile(1, r)
+        for b in range(2, B):
+            load_vk(b)
+            load_q_heads(b, 0)
+            load_q_heads(b, 1)
 
         ident_bf = keep.tile([P, P], BF16, name="ident_bf")
         make_identity(nc, ident_bf[:])
@@ -178,6 +115,7 @@ def tile_lineartransformerblock_pc_kernel(tc, q_feat, vk, k_sum, Wo_words, Wo_sc
             out=order_n[:].rearrange("p (u j e) -> p u j e", u=2, j=32, e=2),
             in_=ident_bf[:].rearrange("p (j u e) -> p u j e", j=32, u=2, e=2),
         )
+
         bias_sb = keep.tile([P, C], F32, name="bias_sb")
         bias_ps = []
 
@@ -189,46 +127,29 @@ def tile_lineartransformerblock_pc_kernel(tc, q_feat, vk, k_sum, Wo_words, Wo_sc
                 )
                 bias_ps.append(bank)
 
-        def spread_half(nh, tag):
-            while len(bias_ps) < 2:
-                bias_ps.append(None)
-            bias_ps[nh] = ps_one.tile([P, N_MX], F32, name="bias_ps", tag=tag)
-            nc.tensor.matmul(
-                out=bias_ps[nh][:], lhsT=ones_bf[:], rhs=bias_row[:, nh * N_MX : (nh + 1) * N_MX], start=True, stop=True
-            )
-
-        def keep_half(nh, on_vector):
-            if on_vector:
-                nc.vector.tensor_copy(out=bias_sb[:, nh * N_MX : (nh + 1) * N_MX], in_=bias_ps[nh][:])
-            else:
+        def keep_bias():
+            for nh in range(N_HALVES):
                 nc.scalar.copy(out=bias_sb[:, nh * N_MX : (nh + 1) * N_MX], in_=bias_ps[nh][:])
-
-        def keep_bias(halves=(0, 1)):
-            for nh in halves:
-                if KB_ACT:
-                    nc.scalar.copy(out=bias_sb[:, nh * N_MX : (nh + 1) * N_MX], in_=bias_ps[nh][:])
-                else:
-                    nc.vector.tensor_copy(out=bias_sb[:, nh * N_MX : (nh + 1) * N_MX], in_=bias_ps[nh][:])
 
         warm = keep.tile([P, 1], F32, name="warm")
         nc.vector.memset(warm[:], 0.0)
         nc.scalar.activation(out=warm[:], in_=warm[:], func=ACT.Copy)
 
+        def matmuls_on_zeros(count):
+            for k in range(count):
+                junk = ps_one.tile([P, N_MX], F32, name="junk", tag="o%d" % (k % N_HALVES))
+                nc.tensor.matmul(out=junk[:], lhsT=zeros[:, 0:P], rhs=zeros[:], start=True, stop=True)
+
         vk_t = keep.tile([P, B * H, VK_PITCH], BF16, name="vk_t")
 
         def transpose_k_sum():
-            if HEAD_BANKS:
-                ks_ps = ps_one.tile([P, H, P], BF16, name="ks_ps", tag=KS_TAG)
-            else:
-                ks_ps = ps_t.tile([P, H, P], BF16, name="ks_ps", tag="t")
+            ks_ps = ps_one.tile([P, H, P], BF16, name="ks_ps", tag="hs2")
             nc.tensor.transpose(out=ks_ps[:, 0, :], in_=ks_sb[:], identity=ident_bf[:])
             nc.vector.tensor_copy(out=vk_t[:, :, D], in_=ks_ps[:, 0, 0 : B * H])
 
         def transpose_vk(b):
-            if HEAD_BANKS and b == 0:
+            if b == 0:
                 vk_ps = ps_one.tile([P, H, P], BF16, name="vk_ps", tag="a")
-            elif b in VK_EARLY:
-                vk_ps = ps_one.tile([P, H, P], BF16, name="vk_ps", tag="o%d" % (b % 2))
             else:
                 vk_ps = ps_t.tile([P, H, P], BF16, name="vk_ps", tag="t")
             for h in range(H):
@@ -236,50 +157,38 @@ def tile_lineartransformerblock_pc_kernel(tc, q_feat, vk, k_sum, Wo_words, Wo_sc
             nc.vector.tensor_copy(out=vk_t[:, b * H : (b + 1) * H, 0:D], in_=vk_ps[:])
 
         q_t = {}
-        q_pss = {}
-        a_pss = {}
         hs_ps = {}
         den_sb = {}
         r_den = {}
         a_sb = {}
+        a_ps = {}
         grouped = {}
         codes = {}
         a_scales = {}
         out_ps = {}
         out_sb = {}
 
-        def transpose_q(i, tag=None):
+        def transpose_q(i):
             b, r = divmod(i, ROWS)
-            if tag:
-                q_ps = ps_one.tile([P, H, P], BF16, name="q_ps", tag=tag)
-            else:
-                q_ps = ps_t.tile([P, H, P], BF16, name="q_ps", tag="t")
+            if r == 0 and b > 0:
+                transpose_vk(b)
+            q_ps = ps_t.tile([P, H, P], BF16, name="q_ps", tag="t")
             for h in range(H):
                 nc.tensor.transpose(out=q_ps[:, h, :], in_=q_sb[b][:, h, r, :], identity=ident_bf[:])
-            q_pss[i] = q_ps
-
-        def copy_q(i, on_vector=False):
-            q_ps = q_pss[i]
             q_t[i] = work.tile([P, H, P], BF16, name="q_t", bufs=TILES)
-            if on_vector or (QCOPY_V and i % QCOPY_V == QCOPY_V - 1) or QV_LO <= i < QV_HI:
+            if Q_AHEAD <= i < Q_AHEAD + LAG:
                 nc.vector.tensor_copy(out=q_t[i][:], in_=q_ps[:])
             else:
                 nc.scalar.copy(out=q_t[i][:], in_=q_ps[:])
 
-        def read_out(i, groups=(0, 1, 2)):
+        def read_out(i, banks):
             b = i // ROWS
-            if 0 in groups:
+            if 0 in banks:
                 hs_ps[i] = []
-            for k in groups:
-                heads = BANK_HEADS[k]
-                if i in ALT_TAGS:
-                    at = ALT_TAGS[i][k]
-                    bank = (ps_t if at == "t" else ps_one).tile([P, 3, HS_PITCH], F32, name="hs_ps", tag=at)
-                elif HS_BUFS == 4:
-                    bank = ps_one.tile([P, 3, HS_PITCH], F32, name="hs_ps", tag="hs", bufs=4)
-                else:
-                    bank = ps_one.tile([P, 3, HS_PITCH], F32, name="hs_ps", tag="hs%d" % k)
-                for slot, h in enumerate(heads):
+            for k in banks:
+                tag = OTHER_BANKS[i][k] if i in OTHER_BANKS else "hs%d" % k
+                bank = (ps_t if tag == "t" else ps_one).tile([P, 3, HS_PITCH], F32, name="hs_ps", tag=tag)
+                for slot, h in enumerate(BANK_HEADS[k]):
                     nc.tensor.matmul(
                         out=bank[:, slot, 0 : D + 1],
                         lhsT=q_t[i][:, h, :],
@@ -289,78 +198,25 @@ def tile_lineartransformerblock_pc_kernel(tc, q_feat, vk, k_sum, Wo_words, Wo_sc
                     )
                 hs_ps[i].append(bank)
 
-        def mm_list(i, groups):
-            b = i // ROWS
-            if 0 in groups:
-                hs_ps[i] = []
-
-            def one(k, slot, h):
-                if slot == 0:
-                    bank = ps_one.tile([P, 3, HS_PITCH], F32, name="hs_ps", tag="hs%d" % k)
-                    hs_ps[i].append(bank)
-                nc.tensor.matmul(
-                    out=hs_ps[i][k][:, slot, 0 : D + 1], lhsT=q_t[i][:, h, :], rhs=vk_t[:, b * H + h, 0 : D + 1], start=True, stop=True
-                )
-
-            return [(one, (k, slot, h)) for k in groups for slot, h in enumerate(BANK_HEADS[k])]
-
-        def tq_list(i):
-            b, r = divmod(i, ROWS)
-
-            def one(h):
-                if h == 0:
-                    q_pss[i] = ps_t.tile([P, H, P], BF16, name="q_ps", tag="t")
-                nc.tensor.transpose(out=q_pss[i][:, h, :], in_=q_sb[b][:, h, r, :], identity=ident_bf[:])
-
-            return [(one, (h,)) for h in range(H)]
-
-        def ta_list(i):
-            def one(g, u):
-                if g == 0 and u == 0:
-                    a_pss[i] = ps_one.tile([P, PASSES, 2, P], F32, name="a_ps", tag="a")
-                nc.tensor.transpose(
-                    out=a_pss[i][:, g, u, :],
-                    in_=a_sb[i][:, g, u, :, :].rearrange("p h w -> p (h w)").bitcast(F32),
-                    identity=ident_f32[:],
-                )
-
-            return [(one, (g, u)) for g in range(PASSES) for u in range(2)]
-
-        def weave(first, second, lead):
-            seq = list(first[:lead])
-            rest = list(first[lead:])
-            other = list(second)
-            while rest or other:
-                if other:
-                    seq.append(other.pop(0))
-                if rest:
-                    seq.append(rest.pop(0))
-            for fn, args in seq:
-                fn(*args)
-
-        def den_add(i, groups=(0, 1, 2)):
-            if 0 in groups:
+        def add_eps(i, banks):
+            if 0 in banks:
                 den_sb[i] = work.tile([P, H], F32, name="den")
-            den = den_sb[i]
-            for k in groups:
-                heads = BANK_HEADS[k]
+            for k in banks:
+                heads = len(BANK_HEADS[k])
                 nc.vector.tensor_scalar_add(
-                    out=den[:, 3 * k : 3 * k + len(heads)], in0=hs_ps[i][k][:, 0 : len(heads), D], scalar1=EPS
+                    out=den_sb[i][:, 3 * k : 3 * k + heads], in0=hs_ps[i][k][:, 0:heads, D], scalar1=EPS
                 )
-            den_sb[i] = den
 
-        def reciprocal(i, groups=(0, 1, 2)):
-            if 0 in groups:
+        def reciprocal(i, banks):
+            if 0 in banks:
                 r_den[i] = work.tile([P, H], F32, name="r_den")
-            if SPLIT_RECIP:
-                for k in groups:
-                    heads = BANK_HEADS[k]
-                    cols = slice(3 * k, 3 * k + len(heads))
-                    nc.vector.reciprocal(out=r_den[i][:, cols], in_=den_sb[i][:, cols])
-            else:
-                nc.vector.reciprocal(out=r_den[i][:], in_=den_sb[i][:])
+            for k in banks:
+                cols = slice(3 * k, 3 * k + len(BANK_HEADS[k]))
+                nc.vector.reciprocal(out=r_den[i][:, cols], in_=den_sb[i][:, cols])
 
-        def norm_scalar(i, k):
+        def scale_on_scalar(i, k):
+            if k == 0:
+                a_sb[i] = work.tile([P, PASSES, 2, HEADS_PER_PASS, D // 2], BF16, name="a_sb")
             for slot, h in enumerate(BANK_HEADS[k]):
                 g, hh = divmod(h, HEADS_PER_PASS)
                 nc.scalar.activation(
@@ -370,48 +226,30 @@ def tile_lineartransformerblock_pc_kernel(tc, q_feat, vk, k_sum, Wo_words, Wo_sc
                     scale=r_den[i][:, 3 * k + slot : 3 * k + slot + 1],
                 )
 
-        def norm_vector(i, k):
-            if k == 1:
-                nc.vector.tensor_tensor(
-                    out=a_sb[i][:, 1, :, 0:3, :].rearrange("p u h w -> p h u w"),
-                    in0=hs_ps[i][1][:, :, 0:D].rearrange("p h (u w) -> p h u w", u=2),
-                    in1=r_den[i][:, 3:6].unsqueeze(2).unsqueeze(3).to_broadcast([P, 3, 2, D // 2]),
-                    op=ALU.mult,
-                )
-            else:
-                nc.vector.tensor_tensor(
-                    out=a_sb[i][:, :, :, 3, :],
-                    in0=hs_ps[i][2][:, 0:2, 0:D].rearrange("p h (u w) -> p h u w", u=2),
-                    in1=r_den[i][:, 6:8].unsqueeze(2).unsqueeze(3).to_broadcast([P, 2, 2, D // 2]),
-                    op=ALU.mult,
-                )
-
-        def new_a(i):
-            a_sb[i] = work.tile([P, PASSES, 2, HEADS_PER_PASS, D // 2], BF16, name="a_sb")
+        def scale_on_vector(i):
+            nc.vector.tensor_tensor(
+                out=a_sb[i][:, 1, :, 0:3, :].rearrange("p u h w -> p h u w"),
+                in0=hs_ps[i][1][:, :, 0:D].rearrange("p h (u w) -> p h u w", u=2),
+                in1=r_den[i][:, 3:6].unsqueeze(2).unsqueeze(3).to_broadcast([P, 3, 2, D // 2]),
+                op=ALU.mult,
+            )
 
         def transpose_a(i):
-            if HS_BUFS == 4:
-                a_ps = ps_t.tile([P, PASSES, 2, P], F32, name="a_ps", tag="t")
-            else:
-                a_ps = ps_one.tile([P, PASSES, 2, P], F32, name="a_ps", tag="a")
+            a_ps[i] = ps_one.tile([P, PASSES, 2, P], F32, name="a_ps", tag="a")
             for g in range(PASSES):
                 for u in range(2):
                     nc.tensor.transpose(
-                        out=a_ps[:, g, u, :],
+                        out=a_ps[i][:, g, u, :],
                         in_=a_sb[i][:, g, u, :, :].rearrange("p h w -> p (h w)").bitcast(F32),
                         identity=ident_f32[:],
                     )
-            a_pss[i] = a_ps
-
-        def copy_a(i, on_vector=False):
-            a_ps = a_pss[i]
             grouped[i] = work.tile([P, PASSES, P, PACK], BF16, name="grouped", align_bytes=64)
-            (nc.vector.tensor_copy if on_vector else nc.scalar.copy)(
+            nc.scalar.copy(
                 out=grouped[i][:]
                 .rearrange("p g s t -> p (g s t)")
                 .bitcast(F32)
                 .rearrange("p (g s u) -> p g s u", g=PASSES, u=2),
-                in_=a_ps[:].rearrange("p g u s -> p g s u"),
+                in_=a_ps[i][:].rearrange("p g u s -> p g s u"),
             )
 
         def quantise(i):
@@ -423,31 +261,10 @@ def tile_lineartransformerblock_pc_kernel(tc, q_feat, vk, k_sum, Wo_words, Wo_sc
                 in_=grouped[i][:].rearrange("p g s t -> p (g s t)"),
             )
 
-        def project(i, halves=(0, 1)):
-            if P_GOUTER and len(halves) == 2:
-                out_ps[i] = [ps_one.tile([P, N_MX], F32, name="acc", tag=("hs%d" if (DRAIN_BANKS and i == TILES - 2) else "o%d") % nh) for nh in halves]
-                for g in range(PASSES):
-                    tokens = slice(g * P, (g + 1) * P)
-                    for nh in halves:
-                        nc.tensor.matmul_mx(
-                            out=out_ps[i][nh][:],
-                            lhsT=codes[i][:, tokens].bitcast(FP8X4),
-                            lhsT_scale=a_scales[i][:, tokens],
-                            rhs=w_words[:, g, nh * N_MX * PACK : (nh + 1) * N_MX * PACK].bitcast(FP8X4),
-                            rhs_scale=w_scales[:, g, nh * N_MX : (nh + 1) * N_MX],
-                            start=(g == 0),
-                            stop=(g == PASSES - 1),
-                        )
-                return
-            if 0 in halves:
-                out_ps[i] = []
-            for nh in halves:
-                if RING_FROM <= 2 * i + nh:
-                    acc = ps_one.tile([P, N_MX], F32, name="acc", tag=("o0", "o1", "hs0", "hs1", "hs2")[(2 * i + nh - RING_FROM) % 5])
-                elif DRAIN_BANKS and i == TILES - 2:
-                    acc = ps_one.tile([P, N_MX], F32, name="acc", tag="hs%d" % nh)
-                else:
-                    acc = ps_one.tile([P, N_MX], F32, name="acc", tag="o%d" % nh)
+        def project(i):
+            out_ps[i] = []
+            for nh in range(N_HALVES):
+                acc = ps_one.tile([P, N_MX], F32, name="acc", tag=("hs%d" if i == TILES - 2 else "o%d") % nh)
                 for g in range(PASSES):
                     tokens = slice(g * P, (g + 1) * P)
                     nc.tensor.matmul_mx(
@@ -465,150 +282,57 @@ def tile_lineartransformerblock_pc_kernel(tc, q_feat, vk, k_sum, Wo_words, Wo_sc
             if nh == 0:
                 out_sb[i] = work.tile([P, C], F32, name="out_sb")
             b, r = divmod(i, ROWS)
-            pieces = TAIL_SPLIT if (i == TILES - 1 and nh >= TAIL_FROM) else 1
-            w = N_MX // pieces
-            for q in range(pieces):
-                cols = slice(nh * N_MX + q * w, nh * N_MX + (q + 1) * w)
-                nc.vector.tensor_tensor(out=out_sb[i][:, cols], in0=out_ps[i][nh][:, q * w : (q + 1) * w], in1=(bias_bc if BIAS_DMA else bias_sb)[:, cols], op=ALU.add)
-                nc.sync.dma_start(out=out[b].rearrange("(p r) c -> r p c", r=ROWS)[r][:, cols], in_=out_sb[i][:, cols])
+            cols = slice(nh * N_MX, (nh + 1) * N_MX)
+            nc.vector.tensor_tensor(out=out_sb[i][:, cols], in0=out_ps[i][nh][:], in1=bias_sb[:, cols], op=ALU.add)
+            nc.sync.dma_start(out=out[b].rearrange("(p r) c -> r p c", r=ROWS)[r][:, cols], in_=out_sb[i][:, cols])
 
-        nq = [0]
+        matmuls_on_zeros(WARM_UP_MATMULS)
+        transpose_q(0)
+        transpose_vk(0)
+        transpose_k_sum()
+        spread_bias()
+        keep_bias()
+        transpose_q(1)
 
-        def tq(i, tag=None):
-            if i % ROWS == 0 and i > 0 and (i // ROWS) not in VK_EARLY:
-                transpose_vk(i // ROWS)
-            transpose_q(i, tag)
-            copy_q(i, tag is not None)
-            if i == 0:
-                warm_up(WARM_HEAD[0], "o1")
-                transpose_vk(0)
-                transpose_k_sum()
-                warm_up(WARM_HEAD[1], "o1")
+        for i in range(LAG):
+            read_out(i, ALL_BANKS)
+            if i == LAG - 1:
+                matmuls_on_zeros(KEEP_WARM_MATMULS)
+            add_eps(i, ALL_BANKS)
+            reciprocal(i, ALL_BANKS)
+            scale_on_scalar(i, 0)
             if i == 1:
-                warm_up(WARM_HEAD[2], "o1")
+                transpose_a(0)
+            scale_on_scalar(i, 2)
+            scale_on_vector(i)
+            if i == 2:
+                quantise(0)
+                transpose_a(1)
+            transpose_q(i + Q_AHEAD)
 
-        def n2(i):
-            if FILL_V5 and (i < FILL_V5 or i >= TILES - 1):
-                norm_vector(i, 2)
-            else:
-                norm_scalar(i, 2)
-
-        STAGE = {
-            "R": read_out, "den": den_add, "rec": reciprocal, "na": new_a,
-            "Ra": lambda i: read_out(i, (0, 1)), "Rb": lambda i: read_out(i, (2,)),
-            "den01": lambda i: den_add(i, (0, 1)), "den2": lambda i: den_add(i, (2,)),
-            "rec01": lambda i: reciprocal(i, (0, 1)), "rec2": lambda i: reciprocal(i, (2,)),
-            "nA0": lambda i: norm_scalar(i, 0), "n2": n2, "nV1": lambda i: norm_vector(i, 1),
-            "TA": transpose_a, "cA": copy_a, "cAV": lambda i: copy_a(i, True), "TQ": tq, "cQ": copy_q, "qz": quantise,
-            "P": project, "P0": lambda i: project(i, (0,)), "P1": lambda i: project(i, (1,)),
-            "b0": lambda i: add_bias_and_store(i, 0), "b1": lambda i: add_bias_and_store(i, 1),
-        }
-        def head():
-            q_t[0] = work.tile([P, H, P], BF16, name="q_t", bufs=TILES)
-            for half, vtag in ((0, "a"), (1, "o1")):
-                q_ps = ps_t.tile([P, 4, P], BF16, name="q_ps", tag="t")
-                for h in range(4):
-                    nc.tensor.transpose(out=q_ps[:, h, :], in_=q_sb[0][:, 4 * half + h, 0, :], identity=ident_bf[:])
-                nc.scalar.copy(out=q_t[0][:, 4 * half : 4 * half + 4, :], in_=q_ps[:])
-                vk_ps = ps_one.tile([P, 4, P], BF16, name="vk_ps", tag=vtag)
-                for h in range(4):
-                    nc.tensor.transpose(out=vk_ps[:, h, :], in_=vk_sb[0][:, 4 * half + h, :], identity=order_n[:])
-                nc.vector.tensor_copy(out=vk_t[:, 4 * half : 4 * half + 4, 0:D], in_=vk_ps[:])
-                if half == 0:
-                    transpose_k_sum()
-
-        warm_up(WARM0)
-        if SEQ:
-            for tok in SEQ.split():
-                n, arg = tok.split(":")
-                if n == "B":
-                    spread_half(int(arg[0]), arg[1:])
-                elif n == "kbA":
-                    keep_half(int(arg), False)
-                elif n == "kbV":
-                    keep_half(int(arg), True)
-                elif n == "TQ":
-                    tq(int(arg))
-                    nq[0] = int(arg) + 1
-                elif n == "W":
-                    warm_up(1, arg)
-                else:
-                    STAGE[n](int(arg))
-        if HEAD_SPLIT:
-            head()
-        for j in range(1 if HEAD_SPLIT else 0, 0 if SEQ else PRO):
-            tq(j)
-            warm_up(WARM1[j], "o1")
-        if not SEQ:
-            nq[0] = PRO
-        maxlag = max(l for (n, l) in TEMPLATE)
-        ph = [0]
-        bh = [0]
-        for i in range(FIRST_STEP, TILES + maxlag + EXTRA_STEPS):
-            for (n, lag) in (TEMPLATE_DRAIN if (TEMPLATE_DRAIN and i >= DRAIN_FROM) else TEMPLATE_FILL if (TEMPLATE_FILL and (i < FILL_STEPS or i >= DRAIN_FROM)) else TEMPLATE):
-                if n == "Q":
-                    if nq[0] < TILES:
-                        tq(nq[0])
-                        nq[0] += 1
-                elif n == "X":
-                    if i < len(XTRA) and XTRA[i] and nq[0] < TILES:
-                        tq(nq[0], XTRA[i])
-                        nq[0] += 1
-                elif n == "WQ":
-                    j = i + WQ_LEAD
-                    ts = []
-                    if j < TILES:
-                        if j % ROWS == 0:
-                            transpose_vk(j // ROWS)
-                        ts = tq_list(j)
-                    ms = mm_list(i, WQ_GROUPS) if i < TILES else []
-                    if WEAVE_END_MM:
-                        weave(ts, ms, max(0, len(ts) - len(ms) + 1) if ms else len(ts))
-                    else:
-                        weave(ts, ms, lag)
-                    nq[0] = max(nq[0], j + 1)
-                elif n == "cQ1":
-                    if i + WQ_LEAD < TILES:
-                        copy_q(i + WQ_LEAD)
-                elif n == "WA":
-                    ms = mm_list(i, (2,)) if i < TILES else []
-                    ts = ta_list(i - 1) if (0 <= i - 1 < TILES and not (LAST_TA_SPLIT and i == TILES)) else []
-                    weave(ms, ts, 1 if ms else 0)
-                elif n == "PH":
-                    count = 2 if (i < SLOW_FROM or i >= SLOW_TO) else 1
-                    for k in range(count):
-                        if ph[0] < 2 * TILES and ph[0] // 2 <= i - lag:
-                            project(ph[0] // 2, (ph[0] % 2,))
-                            ph[0] += 1
-                elif n == "BH":
-                    if bh[0] < ph[0]:
-                        add_bias_and_store(bh[0] // 2, bh[0] % 2)
-                        bh[0] += 1
-                elif n == "VK":
-                    for bb in VK_EARLY:
-                        if VK_EARLY[bb] == i:
-                            transpose_vk(bb)
-                elif n == "bias":
-                    if i == lag and not BIAS_DMA:
-                        spread_bias()
-                elif n == "kbias":
-                    if i == lag and not BIAS_DMA:
-                        keep_bias()
-                elif n == "kb0":
-                    if i == lag and not BIAS_DMA:
-                        keep_bias((0,))
-                elif n == "kb1":
-                    if i == lag and not BIAS_DMA:
-                        keep_bias((1,))
-                elif n == "W":
-                    if i < len(WARM_FILL):
-                        warm_up(WARM_FILL[i][lag], "o0")
-                elif LAST_TA_SPLIT and i == TILES and n == "P":
-                    project(i - lag, (0,))
-                    transpose_a(TILES - 1)
-                    copy_a(TILES - 1)
-                    project(i - lag, (1,))
-                elif LAST_TA_SPLIT and i == TILES and n in ("TA", "cA"):
-                    pass
-                elif 0 <= i - lag < TILES:
-                    STAGE[n](i - lag)
+        for i in range(LAG, TILES + LAG):
+            reads = i < TILES
+            if reads:
+                read_out(i, (0, 1))
+                add_eps(i, (0, 1))
+            project(i - LAG)
+            if reads:
+                read_out(i, (2,))
+            if i - 2 < TILES:
+                quantise(i - 2)
+            if reads:
+                reciprocal(i, (0, 1))
+                scale_on_scalar(i, 0)
+            add_bias_and_store(i - LAG, 0)
+            if reads:
+                scale_on_vector(i)
+                add_eps(i, (2,))
+            add_bias_and_store(i - LAG, 1)
+            if reads:
+                reciprocal(i, (2,))
+            if i - 1 < TILES:
+                transpose_a(i - 1)
+            if reads:
+                scale_on_scalar(i, 2)
+            if i + Q_AHEAD < TILES:
+                transpose_q(i + Q_AHEAD)

@@ -280,7 +280,7 @@ def tile_lineartransformerblock_pc_kernel(tc, q_feat, vk, k_sum, Wo_words, Wo_sc
 
         def add_bias_and_store(i, nh):
             if nh == 0:
-                out_sb[i] = work.tile([P, C], F32, name="out_sb")
+                out_sb[i] = work.tile([P, C], F32, name="out_sb", bufs=TILES)
             b, r = divmod(i, ROWS)
             cols = slice(nh * N_MX, (nh + 1) * N_MX)
             nc.vector.tensor_tensor(out=out_sb[i][:, cols], in0=out_ps[i][nh][:], in1=bias_sb[:, cols], op=ALU.add)

@@ -24,6 +24,7 @@ N_MX = 512
 N_HALVES = C // N_MX
 ROWS = S // P
 TILES = B * ROWS
+PAIRED = (2, 3)
 VK_PITCH = 136
 
 HS_PITCH = D + 2
@@ -34,7 +35,7 @@ LAG = 3
 Q_AHEAD = 2
 WARM_UP_MATMULS = 6
 KEEP_WARM_MATMULS = 2
-OTHER_BANKS = {1: ("o0", "o1", "t"), TILES - 1: ("t", "t", "hs2")}
+OTHER_BANKS = {1: ("o0", "o1", "t")}
 
 FLOPS = 2 * B * S * (H * D) * C + 2 * B * H * S * D * D + 2 * B * H * S * D
 
@@ -44,7 +45,7 @@ def tile_lineartransformerblock_pc_kernel(tc, q_feat, vk, k_sum, Wo_words, Wo_sc
     with ExitStack() as ctx:
         keep = ctx.enter_context(tc.tile_pool(name="keep", bufs=1))
         work = ctx.enter_context(tc.tile_pool(name="work", bufs=4))
-        ps_t = ctx.enter_context(tc.psum_pool(name="ps_t", bufs=2))
+        ps_t = ctx.enter_context(tc.psum_pool(name="ps_t", bufs=5))
         ps_one = ctx.enter_context(tc.psum_pool(name="ps_one", bufs=1))
         ctx.enter_context(tc.manual_schedule())
 
@@ -76,7 +77,12 @@ def tile_lineartransformerblock_pc_kernel(tc, q_feat, vk, k_sum, Wo_words, Wo_sc
             )
 
         def load_vk(b):
-            nc.sync.dma_start(out=vk_sb[b][:], in_=vk[b].rearrange("h n d -> n h d"))
+            if b == 0:
+                nc.sync.dma_start(out=vk_sb[b][:], in_=vk[b].rearrange("h n d -> n h d"))
+            else:
+                nc.sync.dma_start(
+                    out=vk_sb[b][:].rearrange("p j d -> p (j d)"), in_=vk[b].rearrange("h (g j) d -> (h g) (j d)", j=8)
+                )
 
         def load_w():
             for quad in range(4):
@@ -99,8 +105,11 @@ def tile_lineartransformerblock_pc_kernel(tc, q_feat, vk, k_sum, Wo_words, Wo_sc
         load_vk(1)
         load_q_tile(1, 0)
         load_w()
-        for r in range(1, ROWS):
-            load_q_tile(1, r)
+        load_q_tile(1, 1)
+        nc.sync.dma_start(
+            out=q_sb[1][:, :, 2:ROWS, :].rearrange("p h r d -> p h (r d)"),
+            in_=q_feat[1].rearrange("h (p r) d -> p h (r d)", r=ROWS)[:, :, 2 * D :],
+        )
         for b in range(2, B):
             load_vk(b)
             load_q_heads(b, 0)
@@ -115,6 +124,34 @@ def tile_lineartransformerblock_pc_kernel(tc, q_feat, vk, k_sum, Wo_words, Wo_sc
             out=order_n[:].rearrange("p (u j e) -> p u j e", u=2, j=32, e=2),
             in_=ident_bf[:].rearrange("p (j u e) -> p u j e", j=32, u=2, e=2),
         )
+
+        q_mix = {b: keep.tile([P, 2, H, D, 2], BF16, name="q_mix%d" % b) for b in PAIRED}
+        def mix_vk(b):
+            vk_mix[b] = keep.tile([P, 4, D, 2], BF16, name="vk_mix%d" % b)
+            nc.gpsimd.tensor_scalar(
+                out=vk_mix[b][:],
+                in0=vk_sb[b][:].rearrange("p (w e) d -> p w d e", e=2),
+                scalar1=1.0,
+                scalar2=0.0,
+                op0=ALU.mult,
+                op1=ALU.add,
+            )
+
+        vk_mix = {}
+        mix_vk(1)
+        for b in PAIRED:
+            mix_vk(b)
+            for half in range(2):
+                heads = slice(half * HEADS_PER_PASS, (half + 1) * HEADS_PER_PASS)
+                for rho in range(2):
+                    nc.gpsimd.tensor_scalar(
+                        out=q_mix[b][:, rho, heads, :, :],
+                        in0=q_sb[b][:, heads, rho::2, :].rearrange("p h e d -> p h d e"),
+                        scalar1=1.0,
+                        scalar2=0.0,
+                        op0=ALU.mult,
+                        op1=ALU.add,
+                    )
 
         bias_sb = keep.tile([P, C], F32, name="bias_sb")
         bias_ps = []
@@ -143,7 +180,7 @@ def tile_lineartransformerblock_pc_kernel(tc, q_feat, vk, k_sum, Wo_words, Wo_sc
         vk_t = keep.tile([P, B * H, VK_PITCH], BF16, name="vk_t")
 
         def transpose_k_sum():
-            ks_ps = ps_one.tile([P, H, P], BF16, name="ks_ps", tag="hs2")
+            ks_ps = ps_t.tile([P, H, P], BF16, name="ks_ps", tag="t")
             nc.tensor.transpose(out=ks_ps[:, 0, :], in_=ks_sb[:], identity=ident_bf[:])
             nc.vector.tensor_copy(out=vk_t[:, :, D], in_=ks_ps[:, 0, 0 : B * H])
 
@@ -151,12 +188,28 @@ def tile_lineartransformerblock_pc_kernel(tc, q_feat, vk, k_sum, Wo_words, Wo_sc
             if b == 0:
                 vk_ps = ps_one.tile([P, H, P], BF16, name="vk_ps", tag="a")
             else:
-                vk_ps = ps_t.tile([P, H, P], BF16, name="vk_ps", tag="t")
+                vk_ps = ps_t.tile([P, 2, 2, P], F32, name="vk_ps", tag="t")
+                for x in range(2):
+                    for u in range(2):
+                        nc.tensor.transpose(
+                            out=vk_ps[:, u, x, :],
+                            in_=vk_mix[b][:, 2 * x + u, :, :].rearrange("p d e -> p (d e)").bitcast(F32),
+                            identity=ident_f32[:],
+                        )
+                for u in range(2):
+                    nc.vector.tensor_copy(
+                        out=vk_t[:, b * H : (b + 1) * H, u * (D // 2) : (u + 1) * (D // 2)]
+                        .bitcast(F32)
+                        .rearrange("p h (g x) -> p h g x", x=2),
+                        in_=vk_ps[:, u, :, :].rearrange("p x (h g) -> p h g x", h=H),
+                    )
+                return
             for h in range(H):
                 nc.tensor.transpose(out=vk_ps[:, h, :], in_=vk_sb[b][:, h, :], identity=order_n[:])
             nc.vector.tensor_copy(out=vk_t[:, b * H : (b + 1) * H, 0:D], in_=vk_ps[:])
 
         q_t = {}
+        q_pair = {}
         hs_ps = {}
         den_sb = {}
         r_den = {}
@@ -168,25 +221,58 @@ def tile_lineartransformerblock_pc_kernel(tc, q_feat, vk, k_sum, Wo_words, Wo_sc
         out_ps = {}
         out_sb = {}
 
+        def transpose_q_pair(i, half):
+            b, rho = i // ROWS, (i % ROWS) // 2
+            heads = slice(half * HEADS_PER_PASS, (half + 1) * HEADS_PER_PASS)
+            q_ps = ps_t.tile([P, HEADS_PER_PASS, P], F32, name="q_ps", tag="t")
+            for hh in range(HEADS_PER_PASS):
+                nc.tensor.transpose(
+                    out=q_ps[:, hh, :],
+                    in_=q_mix[b][:, rho, half * HEADS_PER_PASS + hh, :, :].rearrange("p d e -> p (d e)").bitcast(F32),
+                    identity=ident_f32[:],
+                )
+            if half == 0:
+                pair = work.tile([P, H, 2, P], BF16, name="q_t_pair", bufs=4)
+                q_t[i] = pair[:, :, 0, :]
+                q_t[i + 1] = pair[:, :, 1, :]
+                q_pair[i] = pair
+            nc.scalar.copy(
+                out=q_pair[i][:, heads, :, :].rearrange("p h t m -> p (h t m)").bitcast(F32),
+                in_=q_ps[:].rearrange("p h s -> p (h s)"),
+            )
+
+        def transpose_q_ahead(i):
+            j = i + Q_AHEAD
+            if j < TILES and j // ROWS not in PAIRED:
+                if j % ROWS == 0:
+                    transpose_vk(j // ROWS)
+                transpose_q(j)
+            if j < TILES and j // ROWS in PAIRED and j % 2 == 0:
+                transpose_q_pair(j, 1)
+            j = i + Q_AHEAD + 1
+            if j < TILES and j // ROWS in PAIRED and j % 2 == 0:
+                if j % ROWS == 0:
+                    transpose_vk(j // ROWS)
+                transpose_q_pair(j, 0)
+
         def transpose_q(i):
             b, r = divmod(i, ROWS)
-            if r == 0 and b > 0:
-                transpose_vk(b)
             q_ps = ps_t.tile([P, H, P], BF16, name="q_ps", tag="t")
             for h in range(H):
                 nc.tensor.transpose(out=q_ps[:, h, :], in_=q_sb[b][:, h, r, :], identity=ident_bf[:])
-            q_t[i] = work.tile([P, H, P], BF16, name="q_t", bufs=TILES)
+            q_sbuf = work.tile([P, H, P], BF16, name="q_t", bufs=TILES - ROWS * len(PAIRED))
+            q_t[i] = q_sbuf[:]
             if Q_AHEAD <= i < Q_AHEAD + LAG:
-                nc.vector.tensor_copy(out=q_t[i][:], in_=q_ps[:])
+                nc.vector.tensor_copy(out=q_t[i], in_=q_ps[:])
             else:
-                nc.scalar.copy(out=q_t[i][:], in_=q_ps[:])
+                nc.scalar.copy(out=q_t[i], in_=q_ps[:])
 
         def read_out(i, banks):
             b = i // ROWS
             if 0 in banks:
                 hs_ps[i] = []
             for k in banks:
-                tag = OTHER_BANKS[i][k] if i in OTHER_BANKS else "hs%d" % k
+                tag = OTHER_BANKS[i][k] if i in OTHER_BANKS else "t"
                 bank = (ps_t if tag == "t" else ps_one).tile([P, 3, HS_PITCH], F32, name="hs_ps", tag=tag)
                 for slot, h in enumerate(BANK_HEADS[k]):
                     nc.tensor.matmul(
@@ -210,9 +296,8 @@ def tile_lineartransformerblock_pc_kernel(tc, q_feat, vk, k_sum, Wo_words, Wo_sc
         def reciprocal(i, banks):
             if 0 in banks:
                 r_den[i] = work.tile([P, H], F32, name="r_den")
-            for k in banks:
-                cols = slice(3 * k, 3 * k + len(BANK_HEADS[k]))
-                nc.vector.reciprocal(out=r_den[i][:, cols], in_=den_sb[i][:, cols])
+            cols = slice(3 * banks[0], 3 * banks[-1] + len(BANK_HEADS[banks[-1]]))
+            nc.vector.reciprocal(out=r_den[i][:, cols], in_=den_sb[i][:, cols])
 
         def scale_on_scalar(i, k):
             if k == 0:
@@ -264,7 +349,7 @@ def tile_lineartransformerblock_pc_kernel(tc, q_feat, vk, k_sum, Wo_words, Wo_sc
         def project(i):
             out_ps[i] = []
             for nh in range(N_HALVES):
-                acc = ps_one.tile([P, N_MX], F32, name="acc", tag=("hs%d" if i == TILES - 2 else "o%d") % nh)
+                acc = (ps_t if i == TILES - 2 else ps_one).tile([P, N_MX], F32, name="acc", tag="t" if i == TILES - 2 else "o%d" % nh)
                 for g in range(PASSES):
                     tokens = slice(g * P, (g + 1) * P)
                     nc.tensor.matmul_mx(
@@ -284,7 +369,12 @@ def tile_lineartransformerblock_pc_kernel(tc, q_feat, vk, k_sum, Wo_words, Wo_sc
             b, r = divmod(i, ROWS)
             cols = slice(nh * N_MX, (nh + 1) * N_MX)
             nc.vector.tensor_tensor(out=out_sb[i][:, cols], in0=out_ps[i][nh][:], in1=bias_sb[:, cols], op=ALU.add)
-            nc.sync.dma_start(out=out[b].rearrange("(p r) c -> r p c", r=ROWS)[r][:, cols], in_=out_sb[i][:, cols])
+            if b in PAIRED:
+                rho, t = divmod(r, 2)
+                rows = out[b].rearrange("(t m r) c -> t r m c", t=2, r=2)[t][rho]
+            else:
+                rows = out[b].rearrange("(p r) c -> r p c", r=ROWS)[r]
+            nc.sync.dma_start(out=rows[:, cols], in_=out_sb[i][:, cols])
 
         matmuls_on_zeros(WARM_UP_MATMULS)
         transpose_q(0)
@@ -308,7 +398,7 @@ def tile_lineartransformerblock_pc_kernel(tc, q_feat, vk, k_sum, Wo_words, Wo_sc
             if i == 2:
                 quantise(0)
                 transpose_a(1)
-            transpose_q(i + Q_AHEAD)
+            transpose_q_ahead(i)
 
         for i in range(LAG, TILES + LAG):
             reads = i < TILES
@@ -334,5 +424,4 @@ def tile_lineartransformerblock_pc_kernel(tc, q_feat, vk, k_sum, Wo_words, Wo_sc
                 transpose_a(i - 1)
             if reads:
                 scale_on_scalar(i, 2)
-            if i + Q_AHEAD < TILES:
-                transpose_q(i + Q_AHEAD)
+            transpose_q_ahead(i)

@@ -33,9 +33,7 @@ ALL_BANKS = (0, 1, 2)
 
 LAG = 3
 Q_AHEAD = 2
-WARM_UP_MATMULS = 6
-KEEP_WARM_MATMULS = 2
-OTHER_BANKS = {1: ("o0", "o1", "t")}
+WARM_UP_MATMULS = 14
 
 FLOPS = 2 * B * S * (H * D) * C + 2 * B * H * S * D * D + 2 * B * H * S * D
 
@@ -45,8 +43,7 @@ def tile_lineartransformerblock_pc_kernel(tc, q_feat, vk, k_sum, Wo_words, Wo_sc
     with ExitStack() as ctx:
         keep = ctx.enter_context(tc.tile_pool(name="keep", bufs=1))
         work = ctx.enter_context(tc.tile_pool(name="work", bufs=4))
-        ps_t = ctx.enter_context(tc.psum_pool(name="ps_t", bufs=5))
-        ps_one = ctx.enter_context(tc.psum_pool(name="ps_one", bufs=1))
+        ps_t = ctx.enter_context(tc.psum_pool(name="ps_t", bufs=8))
         ctx.enter_context(tc.manual_schedule())
 
         q_sb = [keep.tile([P, H, ROWS, D], BF16, name="q_sb%d" % b) for b in range(B)]
@@ -56,17 +53,23 @@ def tile_lineartransformerblock_pc_kernel(tc, q_feat, vk, k_sum, Wo_words, Wo_sc
         w_words = keep.tile([P, PASSES, C * PACK], U8, name="w_words", align_bytes=64)
         w_scales = keep.tile([P, PASSES, C], U8, name="w_scales", align_bytes=64)
         ones_bf = keep.tile([P, P], BF16, name="ones_bf")
-        zeros = keep.tile([P, N_MX], BF16, name="zeros")
+        zeros = keep.tile([P, P], BF16, name="zeros")
 
         nc.vector.memset(zeros[:], 0.0)
+        nc.vector.memset(ks_sb[:], 0.0)
         nc.vector.memset(ones_bf[:], 1.0)
         nc.vector.memset(bias_row[:], 0.0)
-        nc.vector.memset(ks_sb[:], 0.0)
         nc.vector.memset(w_scales[:].rearrange("p g n -> p (g n)").bitcast(I32), 0)
 
         def load_q_tile(b, r):
             nc.sync.dma_start(
                 out=q_sb[b][:, :, r, :], in_=q_feat[b].rearrange("h (p r) d -> r p h d", r=ROWS)[r]
+            )
+
+        def load_q_rest(b):
+            nc.sync.dma_start(
+                out=q_sb[b][:, :, 2:ROWS, :].rearrange("p h r d -> p h (r d)"),
+                in_=q_feat[b].rearrange("h (p r) d -> p h (r d)", r=ROWS)[:, :, 2 * D :],
             )
 
         def load_q_heads(b, half):
@@ -77,12 +80,9 @@ def tile_lineartransformerblock_pc_kernel(tc, q_feat, vk, k_sum, Wo_words, Wo_sc
             )
 
         def load_vk(b):
-            if b == 0:
-                nc.sync.dma_start(out=vk_sb[b][:], in_=vk[b].rearrange("h n d -> n h d"))
-            else:
-                nc.sync.dma_start(
-                    out=vk_sb[b][:].rearrange("p j d -> p (j d)"), in_=vk[b].rearrange("h (g j) d -> (h g) (j d)", j=8)
-                )
+            nc.sync.dma_start(
+                out=vk_sb[b][:].rearrange("p j d -> p (j d)"), in_=vk[b].rearrange("h (g j) d -> (h g) (j d)", j=8)
+            )
 
         def load_w():
             for quad in range(4):
@@ -96,20 +96,17 @@ def tile_lineartransformerblock_pc_kernel(tc, q_feat, vk, k_sum, Wo_words, Wo_sc
                     in_=Wo_words[g].rearrange("p n t -> p (n t)").bitcast(I32),
                 )
 
-        load_q_tile(0, 0)
         load_vk(0)
         nc.sync.dma_start(out=ks_sb[0 : B * H, :], in_=k_sum.rearrange("b h d -> (b h) d"))
+        load_q_tile(0, 0)
         nc.sync.dma_start(out=bias_row[0:1, :], in_=bo.rearrange("(o c) -> o c", o=1))
-        for r in range(1, ROWS):
-            load_q_tile(0, r)
+        load_q_tile(0, 1)
+        load_q_rest(0)
         load_vk(1)
         load_q_tile(1, 0)
         load_w()
         load_q_tile(1, 1)
-        nc.sync.dma_start(
-            out=q_sb[1][:, :, 2:ROWS, :].rearrange("p h r d -> p h (r d)"),
-            in_=q_feat[1].rearrange("h (p r) d -> p h (r d)", r=ROWS)[:, :, 2 * D :],
-        )
+        load_q_rest(1)
         for b in range(2, B):
             load_vk(b)
             load_q_heads(b, 0)
@@ -119,12 +116,6 @@ def tile_lineartransformerblock_pc_kernel(tc, q_feat, vk, k_sum, Wo_words, Wo_sc
         make_identity(nc, ident_bf[:])
         ident_f32 = keep.tile([P, P], F32, name="ident_f32")
         make_identity(nc, ident_f32[:])
-        order_n = keep.tile([P, P], BF16, name="order_n")
-        nc.vector.tensor_copy(
-            out=order_n[:].rearrange("p (u j e) -> p u j e", u=2, j=32, e=2),
-            in_=ident_bf[:].rearrange("p (j u e) -> p u j e", j=32, u=2, e=2),
-        )
-
         q_mix = {b: keep.tile([P, 2, H, D, 2], BF16, name="q_mix%d" % b) for b in PAIRED}
         def mix_vk(b):
             vk_mix[b] = keep.tile([P, 4, D, 2], BF16, name="vk_mix%d" % b)
@@ -158,7 +149,7 @@ def tile_lineartransformerblock_pc_kernel(tc, q_feat, vk, k_sum, Wo_words, Wo_sc
 
         def spread_bias():
             for nh in range(N_HALVES):
-                bank = ps_one.tile([P, N_MX], F32, name="bias_ps", tag="o%d" % nh)
+                bank = ps_t.tile([P, N_MX], F32, name="bias_ps", tag="t")
                 nc.tensor.matmul(
                     out=bank[:], lhsT=ones_bf[:], rhs=bias_row[:, nh * N_MX : (nh + 1) * N_MX], start=True, stop=True
                 )
@@ -166,7 +157,7 @@ def tile_lineartransformerblock_pc_kernel(tc, q_feat, vk, k_sum, Wo_words, Wo_sc
 
         def keep_bias():
             for nh in range(N_HALVES):
-                nc.scalar.copy(out=bias_sb[:, nh * N_MX : (nh + 1) * N_MX], in_=bias_ps[nh][:])
+                nc.vector.tensor_copy(out=bias_sb[:, nh * N_MX : (nh + 1) * N_MX], in_=bias_ps[nh][:])
 
         warm = keep.tile([P, 1], F32, name="warm")
         nc.vector.memset(warm[:], 0.0)
@@ -174,8 +165,11 @@ def tile_lineartransformerblock_pc_kernel(tc, q_feat, vk, k_sum, Wo_words, Wo_sc
 
         def matmuls_on_zeros(count):
             for k in range(count):
-                junk = ps_one.tile([P, N_MX], F32, name="junk", tag="o%d" % (k % N_HALVES))
-                nc.tensor.matmul(out=junk[:], lhsT=zeros[:, 0:P], rhs=zeros[:], start=True, stop=True)
+                if k % 4 == 0:
+                    junk = ps_t.tile([P, N_MX], F32, name="junk", tag="t")
+                nc.tensor.matmul(
+                    out=junk[:, k % 4 * P : (k % 4 + 1) * P], lhsT=zeros[:], rhs=zeros[:], start=True, stop=True
+                )
 
         vk_t = keep.tile([P, B * H, VK_PITCH], BF16, name="vk_t")
 
@@ -185,9 +179,7 @@ def tile_lineartransformerblock_pc_kernel(tc, q_feat, vk, k_sum, Wo_words, Wo_sc
             nc.vector.tensor_copy(out=vk_t[:, :, D], in_=ks_ps[:, 0, 0 : B * H])
 
         def transpose_vk(b):
-            if b == 0:
-                vk_ps = ps_one.tile([P, H, P], BF16, name="vk_ps", tag="a")
-            else:
+            if b > 0:
                 vk_ps = ps_t.tile([P, 2, 2, P], F32, name="vk_ps", tag="t")
                 for x in range(2):
                     for u in range(2):
@@ -204,9 +196,19 @@ def tile_lineartransformerblock_pc_kernel(tc, q_feat, vk, k_sum, Wo_words, Wo_sc
                         in_=vk_ps[:, u, :, :].rearrange("p x (h g) -> p h g x", h=H),
                     )
                 return
-            for h in range(H):
-                nc.tensor.transpose(out=vk_ps[:, h, :], in_=vk_sb[b][:, h, :], identity=order_n[:])
-            nc.vector.tensor_copy(out=vk_t[:, b * H : (b + 1) * H, 0:D], in_=vk_ps[:])
+            for u in range(2):
+                vk_half = ps_t.tile([P, 4, P], BF16, name="vk_half", tag="t")
+                for x in range(2):
+                    for e in range(2):
+                        nc.tensor.transpose(
+                            out=vk_half[:, 2 * x + e, :], in_=vk_sb[b][:, 4 * x + 2 * u + e, :], identity=ident_bf[:]
+                        )
+                (nc.vector.tensor_copy if u == 0 else nc.scalar.copy)(
+                    out=vk_t[:, b * H : (b + 1) * H, u * (D // 2) : (u + 1) * (D // 2)].rearrange(
+                        "p h (g f) -> p h g f", f=4
+                    ),
+                    in_=vk_half[:].rearrange("p f (h g) -> p h g f", h=H),
+                )
 
         q_t = {}
         q_pair = {}
@@ -255,6 +257,18 @@ def tile_lineartransformerblock_pc_kernel(tc, q_feat, vk, k_sum, Wo_words, Wo_sc
                     transpose_vk(j // ROWS)
                 transpose_q_pair(j, 0)
 
+        def transpose_q_first():
+            q_sbuf = work.tile([P, H, P], BF16, name="q_t", bufs=TILES - ROWS * len(PAIRED))
+            q_t[0] = q_sbuf[:]
+            for half in range(2):
+                heads = slice(half * HEADS_PER_PASS, (half + 1) * HEADS_PER_PASS)
+                q_half = ps_t.tile([P, HEADS_PER_PASS, P], BF16, name="q_half", tag="t")
+                for hh in range(HEADS_PER_PASS):
+                    nc.tensor.transpose(
+                        out=q_half[:, hh, :], in_=q_sb[0][:, half * HEADS_PER_PASS + hh, 0, :], identity=ident_bf[:]
+                    )
+                (nc.vector.tensor_copy if half == 0 else nc.scalar.copy)(out=q_t[0][:, heads, :], in_=q_half[:])
+
         def transpose_q(i):
             b, r = divmod(i, ROWS)
             q_ps = ps_t.tile([P, H, P], BF16, name="q_ps", tag="t")
@@ -272,8 +286,7 @@ def tile_lineartransformerblock_pc_kernel(tc, q_feat, vk, k_sum, Wo_words, Wo_sc
             if 0 in banks:
                 hs_ps[i] = []
             for k in banks:
-                tag = OTHER_BANKS[i][k] if i in OTHER_BANKS else "t"
-                bank = (ps_t if tag == "t" else ps_one).tile([P, 3, HS_PITCH], F32, name="hs_ps", tag=tag)
+                bank = ps_t.tile([P, 3, HS_PITCH], F32, name="hs_ps", tag="t")
                 for slot, h in enumerate(BANK_HEADS[k]):
                     nc.tensor.matmul(
                         out=bank[:, slot, 0 : D + 1],
@@ -320,7 +333,7 @@ def tile_lineartransformerblock_pc_kernel(tc, q_feat, vk, k_sum, Wo_words, Wo_sc
             )
 
         def transpose_a(i):
-            a_ps[i] = ps_one.tile([P, PASSES, 2, P], F32, name="a_ps", tag="a")
+            a_ps[i] = ps_t.tile([P, PASSES, 2, P], F32, name="a_ps", tag="t")
             for g in range(PASSES):
                 for u in range(2):
                     nc.tensor.transpose(
@@ -349,7 +362,7 @@ def tile_lineartransformerblock_pc_kernel(tc, q_feat, vk, k_sum, Wo_words, Wo_sc
         def project(i):
             out_ps[i] = []
             for nh in range(N_HALVES):
-                acc = (ps_t if i == TILES - 2 else ps_one).tile([P, N_MX], F32, name="acc", tag="t" if i == TILES - 2 else "o%d" % nh)
+                acc = ps_t.tile([P, N_MX], F32, name="acc", tag="t")
                 for g in range(PASSES):
                     tokens = slice(g * P, (g + 1) * P)
                     nc.tensor.matmul_mx(
@@ -377,17 +390,15 @@ def tile_lineartransformerblock_pc_kernel(tc, q_feat, vk, k_sum, Wo_words, Wo_sc
             nc.sync.dma_start(out=rows[:, cols], in_=out_sb[i][:, cols])
 
         matmuls_on_zeros(WARM_UP_MATMULS)
-        transpose_q(0)
         transpose_vk(0)
         transpose_k_sum()
+        transpose_q_first()
         spread_bias()
         keep_bias()
         transpose_q(1)
 
         for i in range(LAG):
             read_out(i, ALL_BANKS)
-            if i == LAG - 1:
-                matmuls_on_zeros(KEEP_WARM_MATMULS)
             add_eps(i, ALL_BANKS)
             reciprocal(i, ALL_BANKS)
             scale_on_scalar(i, 0)
@@ -397,28 +408,32 @@ def tile_lineartransformerblock_pc_kernel(tc, q_feat, vk, k_sum, Wo_words, Wo_sc
             scale_on_vector(i)
             if i == 2:
                 quantise(0)
-                transpose_a(1)
             transpose_q_ahead(i)
+            if i == 2:
+                transpose_a(1)
 
         for i in range(LAG, TILES + LAG):
             reads = i < TILES
+            last = i == TILES - 1
+            first_banks = ALL_BANKS if last else (0, 1)
             if reads:
-                read_out(i, (0, 1))
-                add_eps(i, (0, 1))
+                read_out(i, first_banks)
+                add_eps(i, first_banks)
             project(i - LAG)
-            if reads:
+            if reads and not last:
                 read_out(i, (2,))
             if i - 2 < TILES:
                 quantise(i - 2)
             if reads:
-                reciprocal(i, (0, 1))
+                reciprocal(i, first_banks)
                 scale_on_scalar(i, 0)
             add_bias_and_store(i - LAG, 0)
             if reads:
                 scale_on_vector(i)
-                add_eps(i, (2,))
+                if not last:
+                    add_eps(i, (2,))
             add_bias_and_store(i - LAG, 1)
-            if reads:
+            if reads and not last:
                 reciprocal(i, (2,))
             if i - 1 < TILES:
                 transpose_a(i - 1)

from contextlib import ExitStack

import concourse.mybir as mybir
from concourse.masks import make_identity

F32 = mybir.dt.float32
BF16 = mybir.dt.bfloat16
I32 = mybir.dt.int32
U32 = mybir.dt.uint32
U8 = mybir.dt.uint8
FP8X4 = mybir.dt.float8_e4m3fn_x4
ALU = mybir.AluOpType
ACT = mybir.ActivationFunctionType

B, H, S, D = 4, 8, 512, 128
C = 1024
P = 128
EPS = 1e-15
PACK = 4
K_PASS = P * PACK
PASSES = H * D // K_PASS
HEADS_PER_PASS = K_PASS // D
N_MX = 512
N_HALVES = C // N_MX
ROWS = S // P
TILES = B * ROWS
PAIRED = (2, 3)
VK_PITCH = 136

HS_PITCH = D + 2
BANK_HEADS = ((0, 1, 2), (4, 5, 6), (3, 7))
ALL_BANKS = (0, 1, 2)

LAG = 3
Q_AHEAD = 2
WARM_UP_MATMULS = 14

FLOPS = 2 * B * S * (H * D) * C + 2 * B * H * S * D * D + 2 * B * H * S * D


def tile_lineartransformerblock_pc_kernel(tc, q_feat, vk, k_sum, Wo_words, Wo_scales, bo, out):
    nc = tc.nc
    with ExitStack() as ctx:
        keep = ctx.enter_context(tc.tile_pool(name="keep", bufs=1))
        work = ctx.enter_context(tc.tile_pool(name="work", bufs=4))
        ps_t = ctx.enter_context(tc.psum_pool(name="ps_t", bufs=8))
        ctx.enter_context(tc.manual_schedule())

        q_sb = [keep.tile([P, H, ROWS, D], BF16, name="q_sb%d" % b) for b in range(B)]
        vk_sb = [keep.tile([P, H, D], BF16, name="vk_sb%d" % b) for b in range(B)]
        ks_sb = keep.tile([P, P], BF16, name="ks_sb")
        bias_row = keep.tile([P, C], BF16, name="bias_row")
        w_words = keep.tile([P, PASSES, C * PACK], U8, name="w_words", align_bytes=64)
        w_scales = keep.tile([P, PASSES, C], U8, name="w_scales", align_bytes=64)
        ones_bf = keep.tile([P, P], BF16, name="ones_bf")
        zeros = keep.tile([P, P], BF16, name="zeros")

        nc.vector.memset(zeros[:], 0.0)
        nc.vector.memset(ks_sb[:], 0.0)
        nc.vector.memset(ones_bf[:], 1.0)
        nc.vector.memset(bias_row[:], 0.0)
        nc.vector.memset(w_scales[:].rearrange("p g n -> p (g n)").bitcast(I32), 0)

        def load_q_tile(b, r):
            nc.sync.dma_start(
                out=q_sb[b][:, :, r, :], in_=q_feat[b].rearrange("h (p r) d -> r p h d", r=ROWS)[r]
            )

        def load_q_rest(b):
            nc.sync.dma_start(
                out=q_sb[b][:, :, 2:ROWS, :].rearrange("p h r d -> p h (r d)"),
                in_=q_feat[b].rearrange("h (p r) d -> p h (r d)", r=ROWS)[:, :, 2 * D :],
            )

        def load_q_heads(b, half):
            heads = slice(half * HEADS_PER_PASS, (half + 1) * HEADS_PER_PASS)
            nc.sync.dma_start(
                out=q_sb[b][:, heads, :, :].rearrange("p h r d -> p h (r d)"),
                in_=q_feat[b, heads].rearrange("h (p r) d -> p h (r d)", r=ROWS),
            )

        def load_vk(b):
            nc.sync.dma_start(
                out=vk_sb[b][:].rearrange("p j d -> p (j d)"), in_=vk[b].rearrange("h (g j) d -> (h g) (j d)", j=8)
            )

        def load_w():
            for quad in range(4):
                nc.sync.dma_start(
                    out=w_scales[32 * quad : 32 * quad + 4, :, :].bitcast(I32),
                    in_=Wo_scales[:, 4 * quad : 4 * quad + 4, :].rearrange("g r n -> r g n").bitcast(I32),
                )
            for g in range(PASSES):
                nc.sync.dma_start(
                    out=w_words[:, g, :].bitcast(I32),
                    in_=Wo_words[g].rearrange("p n t -> p (n t)").bitcast(I32),
                )

        load_vk(0)
        nc.sync.dma_start(out=ks_sb[0 : B * H, :], in_=k_sum.rearrange("b h d -> (b h) d"))
        load_q_tile(0, 0)
        nc.sync.dma_start(out=bias_row[0:1, :], in_=bo.rearrange("(o c) -> o c", o=1))
        load_q_tile(0, 1)
        load_q_rest(0)
        load_vk(1)
        load_q_tile(1, 0)
        load_w()
        load_q_tile(1, 1)
        load_q_rest(1)
        for b in range(2, B):
            load_vk(b)
            load_q_heads(b, 0)
            load_q_heads(b, 1)

        ident_bf = keep.tile([P, P], BF16, name="ident_bf")
        make_identity(nc, ident_bf[:])
        ident_f32 = keep.tile([P, P], F32, name="ident_f32")
        make_identity(nc, ident_f32[:])
        q_mix = {b: keep.tile([P, 2, H, D, 2], BF16, name="q_mix%d" % b) for b in PAIRED}
        def mix_vk(b):
            vk_mix[b] = keep.tile([P, 4, D, 2], BF16, name="vk_mix%d" % b)
            nc.gpsimd.tensor_scalar(
                out=vk_mix[b][:],
                in0=vk_sb[b][:].rearrange("p (w e) d -> p w d e", e=2),
                scalar1=1.0,
                scalar2=0.0,
                op0=ALU.mult,
                op1=ALU.add,
            )

        vk_mix = {}
        mix_vk(1)
        for b in PAIRED:
            mix_vk(b)
            for half in range(2):
                heads = slice(half * HEADS_PER_PASS, (half + 1) * HEADS_PER_PASS)
                for rho in range(2):
                    nc.gpsimd.tensor_scalar(
                        out=q_mix[b][:, rho, heads, :, :],
                        in0=q_sb[b][:, heads, rho::2, :].rearrange("p h e d -> p h d e"),
                        scalar1=1.0,
                        scalar2=0.0,
                        op0=ALU.mult,
                        op1=ALU.add,
                    )

        bias_sb = keep.tile([P, C], F32, name="bias_sb")
        bias_ps = []

        def spread_bias():
            for nh in range(N_HALVES):
                bank = ps_t.tile([P, N_MX], F32, name="bias_ps", tag="t")
                nc.tensor.matmul(
                    out=bank[:], lhsT=ones_bf[:], rhs=bias_row[:, nh * N_MX : (nh + 1) * N_MX], start=True, stop=True
                )
                bias_ps.append(bank)

        def keep_bias():
            for nh in range(N_HALVES):
                nc.vector.tensor_copy(out=bias_sb[:, nh * N_MX : (nh + 1) * N_MX], in_=bias_ps[nh][:])

        warm = keep.tile([P, 1], F32, name="warm")
        nc.vector.memset(warm[:], 0.0)
        nc.scalar.activation(out=warm[:], in_=warm[:], func=ACT.Copy)

        def matmuls_on_zeros(count):
            for k in range(count):
                if k % 4 == 0:
                    junk = ps_t.tile([P, N_MX], F32, name="junk", tag="t")
                nc.tensor.matmul(
                    out=junk[:, k % 4 * P : (k % 4 + 1) * P], lhsT=zeros[:], rhs=zeros[:], start=True, stop=True
                )

        vk_t = keep.tile([P, B * H, VK_PITCH], BF16, name="vk_t")

        def transpose_k_sum():
            ks_ps = ps_t.tile([P, H, P], BF16, name="ks_ps", tag="t")
            nc.tensor.transpose(out=ks_ps[:, 0, :], in_=ks_sb[:], identity=ident_bf[:])
            nc.vector.tensor_copy(out=vk_t[:, :, D], in_=ks_ps[:, 0, 0 : B * H])

        def transpose_vk(b):
            if b > 0:
                vk_ps = ps_t.tile([P, 2, 2, P], F32, name="vk_ps", tag="t")
                for x in range(2):
                    for u in range(2):
                        nc.tensor.transpose(
                            out=vk_ps[:, u, x, :],
                            in_=vk_mix[b][:, 2 * x + u, :, :].rearrange("p d e -> p (d e)").bitcast(F32),
                            identity=ident_f32[:],
                        )
                for u in range(2):
                    nc.vector.tensor_copy(
                        out=vk_t[:, b * H : (b + 1) * H, u * (D // 2) : (u + 1) * (D // 2)]
                        .bitcast(F32)
                        .rearrange("p h (g x) -> p h g x", x=2),
                        in_=vk_ps[:, u, :, :].rearrange("p x (h g) -> p h g x", h=H),
                    )
                return
            for u in range(2):
                vk_half = ps_t.tile([P, 4, P], BF16, name="vk_half", tag="t")
                for x in range(2):
                    for e in range(2):
                        nc.tensor.transpose(
                            out=vk_half[:, 2 * x + e, :], in_=vk_sb[b][:, 4 * x + 2 * u + e, :], identity=ident_bf[:]
                        )
                (nc.vector.tensor_copy if u == 0 else nc.scalar.copy)(
                    out=vk_t[:, b * H : (b + 1) * H, u * (D // 2) : (u + 1) * (D // 2)].rearrange(
                        "p h (g f) -> p h g f", f=4
                    ),
                    in_=vk_half[:].rearrange("p f (h g) -> p h g f", h=H),
                )

        q_t = {}
        q_pair = {}
        hs_ps = {}
        den_sb = {}
        r_den = {}
        a_sb = {}
        a_ps = {}
        grouped = {}
        codes = {}
        a_scales = {}
        out_ps = {}
        out_sb = {}

        def transpose_q_pair(i, half):
            b, rho = i // ROWS, (i % ROWS) // 2
            heads = slice(half * HEADS_PER_PASS, (half + 1) * HEADS_PER_PASS)
            q_ps = ps_t.tile([P, HEADS_PER_PASS, P], F32, name="q_ps", tag="t")
            for hh in range(HEADS_PER_PASS):
                nc.tensor.transpose(
                    out=q_ps[:, hh, :],
                    in_=q_mix[b][:, rho, half * HEADS_PER_PASS + hh, :, :].rearrange("p d e -> p (d e)").bitcast(F32),
                    identity=ident_f32[:],
                )
            if half == 0:
                pair = work.tile([P, H, 2, P], BF16, name="q_t_pair", bufs=4)
                q_t[i] = pair[:, :, 0, :]
                q_t[i + 1] = pair[:, :, 1, :]
                q_pair[i] = pair
            nc.scalar.copy(
                out=q_pair[i][:, heads, :, :].rearrange("p h t m -> p (h t m)").bitcast(F32),
                in_=q_ps[:].rearrange("p h s -> p (h s)"),
            )

        def transpose_q_ahead(i):
            j = i + Q_AHEAD
            if j < TILES and j // ROWS not in PAIRED:
                if j % ROWS == 0:
                    transpose_vk(j // ROWS)
                transpose_q(j)
            if j < TILES and j // ROWS in PAIRED and j % 2 == 0:
                transpose_q_pair(j, 1)
            j = i + Q_AHEAD + 1
            if j < TILES and j // ROWS in PAIRED and j % 2 == 0:
                if j % ROWS == 0:
                    transpose_vk(j // ROWS)
                transpose_q_pair(j, 0)

        def transpose_q_first():
            q_sbuf = work.tile([P, H, P], BF16, name="q_t", bufs=TILES - ROWS * len(PAIRED))
            q_t[0] = q_sbuf[:]
            for half in range(2):
                heads = slice(half * HEADS_PER_PASS, (half + 1) * HEADS_PER_PASS)
                q_half = ps_t.tile([P, HEADS_PER_PASS, P], BF16, name="q_half", tag="t")
                for hh in range(HEADS_PER_PASS):
                    nc.tensor.transpose(
                        out=q_half[:, hh, :], in_=q_sb[0][:, half * HEADS_PER_PASS + hh, 0, :], identity=ident_bf[:]
                    )
                (nc.vector.tensor_copy if half == 0 else nc.scalar.copy)(out=q_t[0][:, heads, :], in_=q_half[:])

        def transpose_q(i):
            b, r = divmod(i, ROWS)
            q_ps = ps_t.tile([P, H, P], BF16, name="q_ps", tag="t")
            for h in range(H):
                nc.tensor.transpose(out=q_ps[:, h, :], in_=q_sb[b][:, h, r, :], identity=ident_bf[:])
            q_sbuf = work.tile([P, H, P], BF16, name="q_t", bufs=TILES - ROWS * len(PAIRED))
            q_t[i] = q_sbuf[:]
            if Q_AHEAD <= i < Q_AHEAD + LAG:
                nc.vector.tensor_copy(out=q_t[i], in_=q_ps[:])
            else:
                nc.scalar.copy(out=q_t[i], in_=q_ps[:])

        def read_out(i, banks):
            b = i // ROWS
            if 0 in banks:
                hs_ps[i] = []
            for k in banks:
                bank = ps_t.tile([P, 3, HS_PITCH], F32, name="hs_ps", tag="t")
                for slot, h in enumerate(BANK_HEADS[k]):
                    nc.tensor.matmul(
                        out=bank[:, slot, 0 : D + 1],
                        lhsT=q_t[i][:, h, :],
                        rhs=vk_t[:, b * H + h, 0 : D + 1],
                        start=True,
                        stop=True,
                    )
                hs_ps[i].append(bank)

        def add_eps(i, banks):
            if 0 in banks:
                den_sb[i] = work.tile([P, H], F32, name="den")
            for k in banks:
                heads = len(BANK_HEADS[k])
                nc.vector.tensor_scalar_add(
                    out=den_sb[i][:, 3 * k : 3 * k + heads], in0=hs_ps[i][k][:, 0:heads, D], scalar1=EPS
                )

        def reciprocal(i, banks):
            if 0 in banks:
                r_den[i] = work.tile([P, H], F32, name="r_den")
            cols = slice(3 * banks[0], 3 * banks[-1] + len(BANK_HEADS[banks[-1]]))
            nc.vector.reciprocal(out=r_den[i][:, cols], in_=den_sb[i][:, cols])

        def scale_on_scalar(i, k):
            if k == 0:
                a_sb[i] = work.tile([P, PASSES, 2, HEADS_PER_PASS, D // 2], BF16, name="a_sb")
            for slot, h in enumerate(BANK_HEADS[k]):
                g, hh = divmod(h, HEADS_PER_PASS)
                nc.scalar.activation(
                    out=a_sb[i][:, g, :, hh, :],
                    in_=hs_ps[i][k][:, slot, 0:D].rearrange("p (u w) -> p u w", u=2),
                    func=ACT.Copy,
                    scale=r_den[i][:, 3 * k + slot : 3 * k + slot + 1],
                )

        def scale_on_vector(i):
            nc.vector.tensor_tensor(
                out=a_sb[i][:, 1, :, 0:3, :].rearrange("p u h w -> p h u w"),
                in0=hs_ps[i][1][:, :, 0:D].rearrange("p h (u w) -> p h u w", u=2),
                in1=r_den[i][:, 3:6].unsqueeze(2).unsqueeze(3).to_broadcast([P, 3, 2, D // 2]),
                op=ALU.mult,
            )

        def transpose_a(i):
            a_ps[i] = ps_t.tile([P, PASSES, 2, P], F32, name="a_ps", tag="t")
            for g in range(PASSES):
                for u in range(2):
                    nc.tensor.transpose(
                        out=a_ps[i][:, g, u, :],
                        in_=a_sb[i][:, g, u, :, :].rearrange("p h w -> p (h w)").bitcast(F32),
                        identity=ident_f32[:],
                    )
            grouped[i] = work.tile([P, PASSES, P, PACK], BF16, name="grouped", align_bytes=64)
            nc.scalar.copy(
                out=grouped[i][:]
                .rearrange("p g s t -> p (g s t)")
                .bitcast(F32)
                .rearrange("p (g s u) -> p g s u", g=PASSES, u=2),
                in_=a_ps[i][:].rearrange("p g u s -> p g s u"),
            )

        def quantise(i):
            codes[i] = work.tile([P, PASSES * P], U32, name="codes", align_bytes=64)
            a_scales[i] = work.tile([P, PASSES * P], U8, name="a_scales", align_bytes=64)
            nc.vector.quantize_mx(
                out=codes[i][:].bitcast(FP8X4),
                scales=a_scales[i][:],
                in_=grouped[i][:].rearrange("p g s t -> p (g s t)"),
            )

        def project(i):
            out_ps[i] = []
            for nh in range(N_HALVES):
                acc = ps_t.tile([P, N_MX], F32, name="acc", tag="t")
                for g in range(PASSES):
                    tokens = slice(g * P, (g + 1) * P)
                    nc.tensor.matmul_mx(
                        out=acc[:],
                        lhsT=codes[i][:, tokens].bitcast(FP8X4),
                        lhsT_scale=a_scales[i][:, tokens],
                        rhs=w_words[:, g, nh * N_MX * PACK : (nh + 1) * N_MX * PACK].bitcast(FP8X4),
                        rhs_scale=w_scales[:, g, nh * N_MX : (nh + 1) * N_MX],
                        start=(g == 0),
                        stop=(g == PASSES - 1),
                    )
                out_ps[i].append(acc)

        def add_bias_and_store(i, nh):
            if nh == 0:
                out_sb[i] = work.tile([P, C], F32, name="out_sb", bufs=TILES)
            b, r = divmod(i, ROWS)
            cols = slice(nh * N_MX, (nh + 1) * N_MX)
            nc.vector.tensor_tensor(out=out_sb[i][:, cols], in0=out_ps[i][nh][:], in1=bias_sb[:, cols], op=ALU.add)
            if b in PAIRED:
                rho, t = divmod(r, 2)
                rows = out[b].rearrange("(t m r) c -> t r m c", t=2, r=2)[t][rho]
            else:
                rows = out[b].rearrange("(p r) c -> r p c", r=ROWS)[r]
            nc.sync.dma_start(out=rows[:, cols], in_=out_sb[i][:, cols])

        matmuls_on_zeros(WARM_UP_MATMULS)
        transpose_vk(0)
        transpose_k_sum()
        transpose_q_first()
        spread_bias()
        keep_bias()
        transpose_q(1)

        for i in range(LAG):
            read_out(i, ALL_BANKS)
            add_eps(i, ALL_BANKS)
            reciprocal(i, ALL_BANKS)
            scale_on_scalar(i, 0)
            if i == 1:
                transpose_a(0)
            scale_on_scalar(i, 2)
            scale_on_vector(i)
            if i == 2:
                quantise(0)
            transpose_q_ahead(i)
            if i == 2:
                transpose_a(1)

        for i in range(LAG, TILES + LAG):
            reads = i < TILES
            last = i == TILES - 1
            first_banks = ALL_BANKS if last else (0, 1)
            if reads:
                read_out(i, first_banks)
                add_eps(i, first_banks)
            project(i - LAG)
            if reads and not last:
                read_out(i, (2,))
            if i - 2 < TILES:
                quantise(i - 2)
            if reads:
                reciprocal(i, first_banks)
                scale_on_scalar(i, 0)
            add_bias_and_store(i - LAG, 0)
            if reads:
                scale_on_vector(i)
                if not last:
                    add_eps(i, (2,))
            add_bias_and_store(i - LAG, 1)
            if reads and not last:
                reciprocal(i, (2,))
            if i - 1 < TILES:
                transpose_a(i - 1)
            if reads:
                scale_on_scalar(i, 2)
            transpose_q_ahead(i)
